import numpy as np
import ml_dtypes


def mxq(x, axis, fmt="e4m3"):
    dtype, down = {"e4m3": (ml_dtypes.float8_e4m3fn, 7), "e5m2": (ml_dtypes.float8_e5m2, 14)}[fmt]
    v = np.moveaxis(np.asarray(x, np.float32).astype(ml_dtypes.bfloat16).astype(np.float64), axis, -1)
    blocks = v.reshape(v.shape[:-1] + (-1, 32))
    amax = np.abs(blocks).max(-1, keepdims=True)
    byte = np.maximum(np.where(amax > 0, np.frexp(amax)[1] - 1 + 127, 0) - down, 1)
    scale = np.exp2(byte - 127.0)
    codes = (blocks / scale).astype(np.float32).astype(dtype).astype(np.float64)
    return np.moveaxis((codes * scale).reshape(v.shape), -1, axis)


WIDE = False


def mx_kscale(k):
    if not WIDE:
        return np.ones(k)
    levels = np.array([10, -10, 5, -5, 0])
    if k % 512:
        return np.exp2(np.random.permutation(np.resize(levels, k // 32))).repeat(32)
    a = np.empty((k // 512, 16))
    for p in range(k // 512):
        a[p, :8] = np.random.permutation(np.resize(levels, 8))
        for g in range(8):
            far = levels[np.abs(levels - a[p, g]) >= 10]
            a[p, g + 8] = far[np.random.randint(len(far))]
    return np.exp2(a.ravel()).repeat(32)


BF16 = ml_dtypes.bfloat16


def bf(x):
    return np.asarray(x, np.float32).astype(BF16)


def f64(x):
    return np.asarray(x).astype(np.float64)


B, D_IN, D_H = 512, 1024, 1024


def sigmoid(v):
    return 1.0 / (1.0 + np.exp(-v))


def setup_inputs():
    s, t = mx_kscale(D_IN), mx_kscale(D_H)
    fg = np.exp(0.75 * np.random.standard_normal((B, D_H)))
    ig = np.exp(0.75 * np.random.standard_normal((B, D_H)))
    c = fg * np.random.standard_normal((B, D_H)) + ig * np.tanh(0.75 * np.random.standard_normal((B, D_H)))
    n = fg * np.random.uniform(size=(B, D_H)) + ig
    return {"x": bf(np.random.standard_normal((B, D_IN)) * s),
            "h_prev": bf(np.random.standard_normal((B, D_H)) * t),
            "c": bf(c),
            "n": bf(n),
            "W_o": bf(np.random.standard_normal((D_IN, D_H)) * 0.5 / np.sqrt(D_IN) / s[:, None]),
            "b_o": bf(np.random.standard_normal(D_H) * 0.3),
            "U_o": bf(np.random.standard_normal((D_H, D_H)) * 0.5 / np.sqrt(D_H) / t[:, None])}


def core(x, h_prev, c, n, W_o, b_o, U_o):
    o = sigmoid((mxq(f64(x), 1, "e4m3") @ mxq(f64(W_o), 0, "e4m3")) + f64(b_o) + (mxq(f64(h_prev), 1, "e4m3") @ mxq(f64(U_o), 0, "e4m3")))
    return o * (f64(c) / (f64(n) + 1e-6))


def e4m3fn_bytes(y):
    return np.clip(np.asarray(y, np.float64), -448.0, 448.0).astype(np.float32).astype(ml_dtypes.float8_e4m3fn).view(np.uint8)


Y_SCALE = 350.0


def reference(x, h_prev, c, n, W_o, b_o, U_o):
    out = core(x, h_prev, c, n, W_o, b_o, U_o)
    return out, e4m3fn_bytes(out * Y_SCALE)

@@ -1,0 +1,272 @@
+from contextlib import ExitStack
+
+import concourse.mybir as mybir
+from concourse.masks import make_identity
+
+F32 = mybir.dt.float32
+BF16 = mybir.dt.bfloat16
+U32 = mybir.dt.uint32
+U8 = mybir.dt.uint8
+FP8X4 = mybir.dt.float8_e4m3fn_x4
+FP8 = mybir.dt.float8_e4m3fn
+ACT = mybir.ActivationFunctionType
+ALU = mybir.AluOpType
+
+P = 128
+FLOPS = 2 * 512 * 2048 * 1024
+Y_SCALE = 350.0
+
+ORDER = (
+    "Ln00 LW00 SU Ln01 LW01 Ln1 LW1 LB Lx0 Lx1 Lh0 Lh1 LW2 LW30 LW31 Lc0 Lc1 LN0 IV0 IS0 LN1 QW0 IV1 IS1 "
+    "LN2 QW1 IV2 IS2 BI TX00 TX10 EV00 TX01 QW2 ES10 TX11 EX0 TX20 EV01 EV11 TX30 EV20 TX21 QX0 ES30 "
+    "TX31 ES21 IV3 IS3 MX02 MX03 MX06 MX00 MX01 MX04 IV4 MX05 IS4 MX12 QW3 MX13 MX16 MX10 MX11 MX14 IV5 "
+    "ES31 MX15 QW4 IS5 MX07 QX1 MX17 CR0 MX22 EX1 MX23 MX26 MX27 MX20 MX21 MX24 MX25 QW5 MX32 MX33 TH2 "
+    "CR1 MX30 MX36 TH3 MX37 MX31 TH7 MX34 MX35 TH4 TO10 TO11 FI10 TH5 FI11 TH1 SA10 TO21 TO20 FI21 CS10 "
+    "SA11 FI20 TH6 SA21 CV11 CS21 SB10 TO30 SA20 CV20 TO31 TH0 FI30 SB11 SB20 SB21 TO01 FI31 CS30 SA30 "
+    "TO00 FI01 SA31 CV31 SB30 CS01 SA01 FI00 SB01 SB31 CV00 SA00 SB00 "
+)
+CHUNKS = ((0, 0, 512), (0, 512, 1024), (1, 0, 1024), (2, 0, 1024), (3, 0, 512), (3, 512, 1024))
+VCOLS = (320, 352, 768, 640, 192, 128)
+LN_UNITS = ((0, 1), (1, 2), (2, 4))
+WSPLIT = (0, 3)
+
+
+def tile_slstmcell_pb_kernel(tc, x, h_prev, c, n, W_o, b_o, U_o, out_0, out_1):
+    nc = tc.nc
+    with ExitStack() as ctx:
+        keep = ctx.enter_context(tc.tile_pool(name="keep", bufs=1))
+        psum = ctx.enter_context(tc.psum_pool(name="psum", bufs=8))
+        ctx.enter_context(tc.manual_schedule())
+
+        rows = {
+            "x": x.rearrange("(p i) k -> p i k", i=4),
+            "h": h_prev.rearrange("(p i) k -> p i k", i=4),
+            "c": c.rearrange("(p i) k -> p i k", i=4),
+            "n": n.rearrange("(p i) k -> p i k", i=4),
+        }
+        wsrc = [
+            W_o[0:512, :].rearrange("(p j) m -> p j m", j=4),
+            W_o[512:1024, :].rearrange("(p j) m -> p j m", j=4),
+            U_o[0:512, :].rearrange("(p j) m -> p j m", j=4),
+            U_o[512:1024, :].rearrange("(p j) m -> p j m", j=4),
+        ]
+        o0 = out_0.rearrange("(p i) m -> p i m", i=4)
+        o1 = out_1.rearrange("(p i) m -> p i m", i=4)
+
+        t = {}
+        for nm in ("x", "h", "c", "n"):
+            for a in range(2):
+                t[nm, a] = keep.tile([P, 2, 1024], BF16, name="%s%d" % (nm, a))
+        raw = {}
+        for g in range(4):
+            if g in WSPLIT:
+                for hh in range(2):
+                    raw[g, hh] = keep.tile([P, 4, 512], BF16, name="raw%d%d" % (g, hh))
+            else:
+                raw[g] = keep.tile([P, 4, 1024], BF16, name="raw%d" % g)
+        wil, wc, ws, where = {}, {}, {}, {}
+        for k in range(len(CHUNKS)):
+            g, c0, c1 = CHUNKS[k]
+            wil[k] = keep.tile([P, c1 - c0, 4], BF16, name="wil%d" % k, align_bytes=64)
+            wc[k] = keep.tile([P, c1 - c0], U32, name="wc%d" % k, align_bytes=64)
+            ws[k] = keep.tile([P, c1 - c0], U8, name="ws%d" % k, align_bytes=64)
+            for ct in range(c0 // P, c1 // P):
+                where[g, ct] = (k, ct * P - c0)
+        xil, xc, xs, lr, crh, ot, hq, f8 = {}, {}, {}, {}, {}, {}, {}, {}
+        for a in range(2):
+            xil[a] = keep.tile([P, 2, 512, 4], BF16, name="xil%d" % a, align_bytes=64)
+            xc[a] = keep.tile([P, 2, 512], U32, name="xc%d" % a, align_bytes=64)
+            xs[a] = keep.tile([P, 2, 512], U8, name="xs%d" % a, align_bytes=64)
+            lr[a] = keep.tile([P, 2, 1024], F32, name="lr%d" % a)
+            crh[a] = keep.tile([P, 2, 1024], F32, name="crh%d" % a)
+        for q in range(4):
+            hq[q] = keep.tile([P, 4, 256], F32, name="hq%d" % q)
+            f8[q] = keep.tile([P, 4, 256], FP8, name="f8%d" % q)
+        for ct in range(8):
+            ot[ct] = keep.tile([P, 512], F32, name="ot%d" % ct)
+        bank = {}
+
+        ident = keep.tile([P, P], F32, name="ident")
+        identb = keep.tile([P, P], BF16, name="identb")
+        bst = keep.tile([P, P], BF16, name="bst")
+        bh = keep.tile([P, 8], F32, name="bh")
+        one = keep.tile([P, 1], F32, name="one")
+        scr = keep.tile([P, 1], F32, name="scr")
+
+        def setup():
+            nc.vector.memset(one[:], 1.0)
+            nc.scalar.activation(out=scr[:], in_=one[:], func=ACT.Ln)
+            nc.gpsimd.memset(bst[:], 0.0)
+            make_identity(nc, ident[:])
+            make_identity(nc, identb[:])
+
+        def load_bias():
+            nc.sync.dma_start(out=bst[0:8, :], in_=b_o.rearrange("(c p) -> c p", p=P))
+
+        def bias():
+            bps = psum.tile([P, P], BF16, name="bps", tag="bank")
+            nc.tensor.transpose(out=bps[:], in_=bst[:], identity=identb[:])
+            nc.vector.tensor_scalar(out=bh[:], in0=bps[:, 0:8], scalar1=0.5, scalar2=None, op0=ALU.mult)
+
+        def load_rows(nm, a, i0, i1):
+            nc.sync.dma_start(out=t[nm, a][:, i0:i1, :], in_=rows[nm][:, 2 * a + i0 : 2 * a + i1, :])
+
+        def load_w(g, hh):
+            if hh is None:
+                nc.sync.dma_start(out=raw[g][:], in_=wsrc[g])
+            else:
+                nc.sync.dma_start(out=raw[g, hh][:], in_=wsrc[g][:, :, 512 * hh : 512 * (hh + 1)])
+
+        def ln(k):
+            i0, i1 = LN_UNITS[k]
+            a = i0 // 2
+            nc.scalar.activation(
+                out=lr[a][:, i0 - 2 * a : i1 - 2 * a, :], in_=t["n", a][:, i0 - 2 * a : i1 - 2 * a, :], func=ACT.Ln, bias=2e-6, scale=2.0
+            )
+
+        def ex(a):
+            nc.scalar.activation(out=lr[a][:], in_=lr[a][:], func=ACT.Exp, scale=-1.0)
+
+        def cr(a):
+            nc.vector.tensor_tensor(out=crh[a][:], in0=t["c", a][:], in1=lr[a][:], op=ALU.mult)
+
+        def tx(g, a):
+            words = t["x" if g < 2 else "h", a][:].rearrange("p i k -> p (i k)").bitcast(F32)
+            ps = psum.tile([P, 2, 2, P], F32, name="tx%d%d" % (g, a), tag="bank")
+            for il in range(2):
+                for u in range(2):
+                    lo = 512 * il + 256 * (g % 2)
+                    nc.tensor.transpose(out=ps[:, il, u, :], in_=words[:, lo + u : lo + 256 : 2], identity=ident[:])
+            bank["tx", g, a] = ps
+
+        def ev(g, a, eng):
+            dst = xil[g // 2][:, g % 2, :, :].rearrange("p b t -> p (b t)").bitcast(F32)[:, 512 * a : 512 * (a + 1)]
+            dst = dst.rearrange("p (i r u) -> p i r u", i=2, u=2)
+            src = bank["tx", g, a][:].rearrange("p i u r -> p i r u")
+            if eng == "V":
+                nc.vector.tensor_copy(out=dst, in_=src)
+            else:
+                nc.scalar.copy(out=dst, in_=src)
+
+        def qx(gp):
+            nc.vector.quantize_mx(
+                out=xc[gp][:].rearrange("p g b -> p (g b)").bitcast(FP8X4),
+                scales=xs[gp][:].rearrange("p g b -> p (g b)"),
+                in_=xil[gp][:].rearrange("p g b t -> p (g b t)"),
+            )
+
+        def il(k, eng):
+            g, c0, c1 = CHUNKS[k]
+            v = VCOLS[k]
+            lo, hi = (0, v) if eng == "V" else (v, c1 - c0)
+            if g in WSPLIT:
+                src = raw[g, c0 // 512][:, :, lo:hi]
+            else:
+                src = raw[g][:, :, c0 + lo : c0 + hi]
+            src = src.rearrange("p j m -> p m j")
+            if eng == "V":
+                nc.vector.tensor_copy(out=wil[k][:, lo:hi, :], in_=src)
+            else:
+                nc.scalar.copy(out=wil[k][:, lo:hi, :], in_=src)
+
+        def qw(k):
+            nc.vector.quantize_mx(out=wc[k][:].bitcast(FP8X4), scales=ws[k][:], in_=wil[k][:].rearrange("p m j -> p (m j)"))
+
+        def mx(g, ct):
+            if g == 0:
+                acc = psum.tile([P, 512], F32, name="acc%d" % ct, tag="bank")
+                bank["acc", ct] = acc
+            k, off = where[g, ct]
+            nc.tensor.matmul_mx(
+                out=bank["acc", ct][:],
+                lhsT=wc[k][:, off : off + P].bitcast(FP8X4),
+                lhsT_scale=ws[k][:, off : off + P],
+                rhs=xc[g // 2][:, g % 2, :].bitcast(FP8X4),
+                rhs_scale=xs[g // 2][:, g % 2, :],
+                start=(g == 0),
+                stop=(g == 3),
+            )
+
+        def th(ct):
+            nc.scalar.activation(out=ot[ct][:], in_=bank["acc", ct][:], func=ACT.Tanh, bias=bh[:, ct : ct + 1], scale=0.5)
+
+        def to(q, a):
+            ps = psum.tile([P, 2, 256], F32, name="to%d%d" % (q, a), tag="bank")
+            for cl in range(2):
+                for il_ in range(2):
+                    i = 2 * a + il_
+                    nc.tensor.transpose(out=ps[:, il_, P * cl : P * (cl + 1)], in_=ot[2 * q + cl][:, P * i : P * (i + 1)], identity=ident[:])
+            bank["to", q, a] = ps
+
+        def fin(q, a):
+            nc.vector.scalar_tensor_tensor(
+                out=hq[q][:, 2 * a : 2 * a + 2, :],
+                in0=bank["to", q, a][:],
+                scalar=1.0,
+                in1=crh[a][:, :, 256 * q : 256 * (q + 1)],
+                op0=ALU.add,
+                op1=ALU.mult,
+            )
+
+        def c8(q, a, eng):
+            dst = f8[q][:, 2 * a : 2 * a + 2, :].rearrange("p i m -> p (i m)")
+            src = hq[q][:, 2 * a : 2 * a + 2, :].rearrange("p i m -> p (i m)")
+            if eng == "V":
+                nc.vector.tensor_scalar(out=dst, in0=src, scalar1=Y_SCALE, scalar2=None, op0=ALU.mult, saturate=False)
+            else:
+                nc.scalar.activation(out=dst, in_=src, func=ACT.Copy, scale=Y_SCALE, saturate=False)
+
+        def st0(q, a):
+            nc.sync.dma_start(out=o0[:, 2 * a : 2 * a + 2, 256 * q : 256 * (q + 1)], in_=hq[q][:, 2 * a : 2 * a + 2, :])
+
+        def st1(q, a):
+            nc.sync.dma_start(out=o1[:, 2 * a : 2 * a + 2, 256 * q : 256 * (q + 1)], in_=f8[q][:, 2 * a : 2 * a + 2, :].bitcast(U8))
+
+        for tok in ORDER.split():
+            op = tok[0:2]
+            d = [int(ch) for ch in tok[2:]]
+            if op == "SU":
+                setup()
+            elif op == "LB":
+                load_bias()
+            elif op == "BI":
+                bias()
+            elif op in ("Lx", "Lh", "Lc", "Ln"):
+                if len(d) == 1:
+                    load_rows(op[1], d[0], 0, 2)
+                else:
+                    load_rows(op[1], d[0], d[1], d[1] + 1)
+            elif op == "LW":
+                load_w(d[0], d[1] if len(d) > 1 else None)
+            elif op == "LN":
+                ln(d[0])
+            elif op == "EX":
+                ex(d[0])
+            elif op == "CR":
+                cr(d[0])
+            elif op == "TX":
+                tx(d[0], d[1])
+            elif op in ("EV", "ES"):
+                ev(d[0], d[1], op[1])
+            elif op == "QX":
+                qx(d[0])
+            elif op in ("IV", "IS"):
+                il(d[0], op[1])
+            elif op == "QW":
+                qw(d[0])
+            elif op == "MX":
+                mx(d[0], d[1])
+            elif op == "TH":
+                th(d[0])
+            elif op == "TO":
+                to(d[0], d[1])
+            elif op == "FI":
+                fin(d[0], d[1])
+            elif op in ("CV", "CS"):
+                c8(d[0], d[1], op[1])
+            elif op == "SA":
+                st0(d[0], d[1])
+            elif op == "SB":
+                st1(d[0], d[1])
+            else:
+                assert False, tok

@@ -17,16 +17,16 @@ FLOPS = 2 * 512 * 2048 * 1024
 Y_SCALE = 350.0
 
 ORDER = (
-    "Ln00 LW00 SU Ln01 LW01 Ln1 LW1 LB Lx0 Lx1 Lh0 Lh1 LW2 LW30 LW31 Lc0 Lc1 LN0 IV0 IS0 LN1 QW0 IV1 IS1 "
-    "LN2 QW1 IV2 IS2 BI TX00 TX10 EV00 TX01 QW2 ES10 TX11 EX0 TX20 EV01 EV11 TX30 EV20 TX21 QX0 ES30 "
-    "TX31 ES21 IV3 IS3 MX02 MX03 MX06 MX00 MX01 MX04 IV4 MX05 IS4 MX12 QW3 MX13 MX16 MX10 MX11 MX14 IV5 "
-    "ES31 MX15 QW4 IS5 MX07 QX1 MX17 CR0 MX22 EX1 MX23 MX26 MX27 MX20 MX21 MX24 MX25 QW5 MX32 MX33 TH2 "
-    "CR1 MX30 MX36 TH3 MX37 MX31 TH7 MX34 MX35 TH4 TO10 TO11 FI10 TH5 FI11 TH1 SA10 TO21 TO20 FI21 CS10 "
-    "SA11 FI20 TH6 SA21 CV11 CS21 SB10 TO30 SA20 CV20 TO31 TH0 FI30 SB11 SB20 SB21 TO01 FI31 CS30 SA30 "
-    "TO00 FI01 SA31 CV31 SB30 CS01 SA01 FI00 SB01 SB31 CV00 SA00 SB00 "
+    "Ln1 LW00 SU Ln00 Ln01 LW01 LW1 LB Lx0 Lx1 Lc1 Lh0 Lh1 LW2 Lc0 LW31 LW30 LN2 IV0 LN0 QW0 LN1 IV1 QW1 "
+    "IV2 EX1 BI TX00 TX10 EV00 TX01 ES10 QW2 ES01 TX11 ES11 CR1 TX20 EX0 TX30 TX21 QX0 TX31 ES20 ES30 "
+    "EV31 MX00 ES21 MX01 IV3 MX02 IS3 MX03 MX04 MX05 MX06 MX07 QX1 MX10 MX11 MX12 MX13 QW3 MX14 IS4 MX15 "
+    "MX16 MX17 IV4 MX20 MX21 IV5 MX22 IS5 QW4 MX23 MX24 MX25 CR0 MX26 MX27 MX30 MX31 TH0 MX32 MX33 TH1 "
+    "QW5 TH2 TO00 TO01 FI00 TH3 MX34 MX35 FI01 TH4 SA00 TO10 CV00 TO11 TH5 SA01 FI10 MX36 CS01 MX37 FI11 "
+    "TO20 SA10 TH6 TO21 FI20 SB00 SA11 TH7 CV10 SA20 CS11 TO30 FI21 SB01 TO31 CS20 SB10 FI30 SB11 SA21 "
+    "FI31 SA30 CV21 CS31 SA31 CV30 SB20 SB21 SB30 SB31 "
 )
 CHUNKS = ((0, 0, 512), (0, 512, 1024), (1, 0, 1024), (2, 0, 1024), (3, 0, 512), (3, 512, 1024))
-VCOLS = (320, 352, 768, 640, 192, 128)
+VCOLS = (512, 512, 1024, 544, 160, 128)
 LN_UNITS = ((0, 1), (1, 2), (2, 4))
 WSPLIT = (0, 3)
 

@@ -163,11 +163,12 @@ def tile_slstmcell_pb_kernel(tc, x, h_prev, c, n, W_o, b_o, U_o, out_0, out_1):
                 src = raw[g, c0 // 512][:, :, lo:hi]
             else:
                 src = raw[g][:, :, c0 + lo : c0 + hi]
-            src = src.rearrange("p j m -> p m j")
+            src = src.rearrange("p t (c i) -> p c t i", i=4)
+            dst = wil[k][:, lo:hi, :].rearrange("p (c i) t -> p c t i", i=4)
             if eng == "V":
-                nc.vector.tensor_copy(out=wil[k][:, lo:hi, :], in_=src)
+                nc.vector.tensor_copy(out=dst, in_=src)
             else:
-                nc.scalar.copy(out=wil[k][:, lo:hi, :], in_=src)
+                nc.scalar.copy(out=dst, in_=src)
 
         def qw(k):
             nc.vector.quantize_mx(out=wc[k][:].bitcast(FP8X4), scales=ws[k][:], in_=wil[k][:].rearrange("p m j -> p (m j)"))

@@ -12,23 +12,18 @@ FP8 = mybir.dt.float8_e4m3fn
 ACT = mybir.ActivationFunctionType
 ALU = mybir.AluOpType
 
-P = 128
-FLOPS = 2 * 512 * 2048 * 1024
+B, D_IN, D_H = 512, 1024, 1024
+FLOPS = 2 * B * (D_IN + D_H) * D_H
 Y_SCALE = 350.0
+EPS = 1e-6
 
-ORDER = (
-    "Ln1 LW00 SU Ln00 Ln01 LW01 LW1 LB Lx0 Lx1 Lc1 Lh0 Lh1 LW2 Lc0 LW31 LW30 LN2 IV0 LN0 QW0 LN1 IV1 QW1 "
-    "IV2 EX1 BI TX00 TX10 EV00 TX01 ES10 QW2 ES01 TX11 ES11 CR1 TX20 EX0 TX30 TX21 QX0 TX31 ES20 ES30 "
-    "EV31 MX00 ES21 MX01 IV3 MX02 IS3 MX03 MX04 MX05 MX06 MX07 QX1 MX10 MX11 MX12 MX13 QW3 MX14 IS4 MX15 "
-    "MX16 MX17 IV4 MX20 MX21 IV5 MX22 IS5 QW4 MX23 MX24 MX25 CR0 MX26 MX27 MX30 MX31 TH0 MX32 MX33 TH1 "
-    "QW5 TH2 TO00 TO01 FI00 TH3 MX34 MX35 FI01 TH4 SA00 TO10 CV00 TO11 TH5 SA01 FI10 MX36 CS01 MX37 FI11 "
-    "TO20 SA10 TH6 TO21 FI20 SB00 SA11 TH7 CV10 SA20 CS11 TO30 FI21 SB01 TO31 CS20 SB10 FI30 SB11 SA21 "
-    "FI31 SA30 CV21 CS31 SA31 CV30 SB20 SB21 SB30 SB31 "
-)
-CHUNKS = ((0, 0, 512), (0, 512, 1024), (1, 0, 1024), (2, 0, 1024), (3, 0, 512), (3, 512, 1024))
-VCOLS = (512, 512, 1024, 544, 160, 128)
-LN_UNITS = ((0, 1), (1, 2), (2, 4))
-WSPLIT = (0, 3)
+P = 128
+PACK = 4
+K_PASS = P * PACK
+SLOTS = B // P
+QUARTER = 2 * P
+
+PIECES = ((0, 0, 512, 0), (0, 512, 1024, 0), (1, 0, 1024, 0), (2, 0, 1024, 480), (3, 0, 512, 352), (3, 512, 1024, 384))
 
 
 def tile_slstmcell_pb_kernel(tc, x, h_prev, c, n, W_o, b_o, U_o, out_0, out_1):
@@ -38,236 +33,267 @@ def tile_slstmcell_pb_kernel(tc, x, h_prev, c, n, W_o, b_o, U_o, out_0, out_1):
         psum = ctx.enter_context(tc.psum_pool(name="psum", bufs=8))
         ctx.enter_context(tc.manual_schedule())
 
-        rows = {
-            "x": x.rearrange("(p i) k -> p i k", i=4),
-            "h": h_prev.rearrange("(p i) k -> p i k", i=4),
-            "c": c.rearrange("(p i) k -> p i k", i=4),
-            "n": n.rearrange("(p i) k -> p i k", i=4),
+        by_slot = {
+            "x": x.rearrange("(p i) k -> p i k", i=SLOTS),
+            "h": h_prev.rearrange("(p i) k -> p i k", i=SLOTS),
+            "c": c.rearrange("(p i) m -> p i m", i=SLOTS),
+            "n": n.rearrange("(p i) m -> p i m", i=SLOTS),
         }
-        wsrc = [
-            W_o[0:512, :].rearrange("(p j) m -> p j m", j=4),
-            W_o[512:1024, :].rearrange("(p j) m -> p j m", j=4),
-            U_o[0:512, :].rearrange("(p j) m -> p j m", j=4),
-            U_o[512:1024, :].rearrange("(p j) m -> p j m", j=4),
+        out_0_by_slot = out_0.rearrange("(p i) m -> p i m", i=SLOTS)
+        out_1_by_slot = out_1.rearrange("(p i) m -> p i m", i=SLOTS)
+        w_pass = [
+            w[K_PASS * half : K_PASS * (half + 1), :].rearrange("(p t) m -> p t m", t=PACK)
+            for w in (W_o, U_o)
+            for half in range(2)
         ]
-        o0 = out_0.rearrange("(p i) m -> p i m", i=4)
-        o1 = out_1.rearrange("(p i) m -> p i m", i=4)
 
-        t = {}
-        for nm in ("x", "h", "c", "n"):
+        rows = {}
+        for name in ("x", "h", "c", "n"):
             for a in range(2):
-                t[nm, a] = keep.tile([P, 2, 1024], BF16, name="%s%d" % (nm, a))
-        raw = {}
-        for g in range(4):
-            if g in WSPLIT:
-                for hh in range(2):
-                    raw[g, hh] = keep.tile([P, 4, 512], BF16, name="raw%d%d" % (g, hh))
-            else:
-                raw[g] = keep.tile([P, 4, 1024], BF16, name="raw%d" % g)
-        wil, wc, ws, where = {}, {}, {}, {}
-        for k in range(len(CHUNKS)):
-            g, c0, c1 = CHUNKS[k]
-            wil[k] = keep.tile([P, c1 - c0, 4], BF16, name="wil%d" % k, align_bytes=64)
-            wc[k] = keep.tile([P, c1 - c0], U32, name="wc%d" % k, align_bytes=64)
-            ws[k] = keep.tile([P, c1 - c0], U8, name="ws%d" % k, align_bytes=64)
-            for ct in range(c0 // P, c1 // P):
-                where[g, ct] = (k, ct * P - c0)
-        xil, xc, xs, lr, crh, ot, hq, f8 = {}, {}, {}, {}, {}, {}, {}, {}
-        for a in range(2):
-            xil[a] = keep.tile([P, 2, 512, 4], BF16, name="xil%d" % a, align_bytes=64)
-            xc[a] = keep.tile([P, 2, 512], U32, name="xc%d" % a, align_bytes=64)
-            xs[a] = keep.tile([P, 2, 512], U8, name="xs%d" % a, align_bytes=64)
-            lr[a] = keep.tile([P, 2, 1024], F32, name="lr%d" % a)
-            crh[a] = keep.tile([P, 2, 1024], F32, name="crh%d" % a)
-        for q in range(4):
-            hq[q] = keep.tile([P, 4, 256], F32, name="hq%d" % q)
-            f8[q] = keep.tile([P, 4, 256], FP8, name="f8%d" % q)
+                rows[name, a] = keep.tile([P, 2, 1024], BF16, name="%s%d" % (name, a))
+        w_raw, w_grouped, w_codes, w_scales, piece_of = {}, {}, {}, {}, {}
+        for k, (g, lo, hi, scalar_cols) in enumerate(PIECES):
+            w_raw[k] = keep.tile([P, PACK, hi - lo], BF16, name="w_raw%d" % k)
+            w_grouped[k] = keep.tile([P, hi - lo, PACK], BF16, name="w_grouped%d" % k, align_bytes=64)
+            w_codes[k] = keep.tile([P, hi - lo], U32, name="w_codes%d" % k, align_bytes=64)
+            w_scales[k] = keep.tile([P, hi - lo], U8, name="w_scales%d" % k, align_bytes=64)
+            for ct in range(lo // P, hi // P):
+                piece_of[g, ct] = (k, ct * P - lo)
+        a_grouped, a_codes, a_scales, recip, ratio = {}, {}, {}, {}, {}
+        for j in range(2):
+            a_grouped[j] = keep.tile([P, 2, B, PACK], BF16, name="a_grouped%d" % j, align_bytes=64)
+            a_codes[j] = keep.tile([P, 2, B], U32, name="a_codes%d" % j, align_bytes=64)
+            a_scales[j] = keep.tile([P, 2, B], U8, name="a_scales%d" % j, align_bytes=64)
+            recip[j] = keep.tile([P, 2, D_H], F32, name="recip%d" % j)
+            ratio[j] = keep.tile([P, 2, D_H], F32, name="ratio%d" % j)
+        tanh_t = {}
         for ct in range(8):
-            ot[ct] = keep.tile([P, 512], F32, name="ot%d" % ct)
+            tanh_t[ct] = keep.tile([P, B], F32, name="tanh_t%d" % ct)
+        h_sb, bytes_sb = {}, {}
+        for q in range(4):
+            h_sb[q] = keep.tile([P, SLOTS, QUARTER], F32, name="h_sb%d" % q)
+            bytes_sb[q] = keep.tile([P, SLOTS, QUARTER], FP8, name="bytes_sb%d" % q)
+        ident_f32 = keep.tile([P, P], F32, name="ident_f32")
+        ident_bf16 = keep.tile([P, P], BF16, name="ident_bf16")
+        bias_rows = keep.tile([P, P], BF16, name="bias_rows")
+        half_bias = keep.tile([P, 8], F32, name="half_bias")
+        one = keep.tile([P, 1], F32, name="one")
+        unused = keep.tile([P, 1], F32, name="unused")
         bank = {}
 
-        ident = keep.tile([P, P], F32, name="ident")
-        identb = keep.tile([P, P], BF16, name="identb")
-        bst = keep.tile([P, P], BF16, name="bst")
-        bh = keep.tile([P, 8], F32, name="bh")
-        one = keep.tile([P, 1], F32, name="one")
-        scr = keep.tile([P, 1], F32, name="scr")
+        def load_rows(name, first, last):
+            a = first // 2
+            nc.sync.dma_start(out=rows[name, a][:, first - 2 * a : last - 2 * a, :], in_=by_slot[name][:, first:last, :])
 
-        def setup():
-            nc.vector.memset(one[:], 1.0)
-            nc.scalar.activation(out=scr[:], in_=one[:], func=ACT.Ln)
-            nc.gpsimd.memset(bst[:], 0.0)
-            make_identity(nc, ident[:])
-            make_identity(nc, identb[:])
+        def load_weights(k):
+            g, lo, hi, scalar_cols = PIECES[k]
+            nc.sync.dma_start(out=w_raw[k][:], in_=w_pass[g][:, :, lo:hi])
 
-        def load_bias():
-            nc.sync.dma_start(out=bst[0:8, :], in_=b_o.rearrange("(c p) -> c p", p=P))
-
-        def bias():
-            bps = psum.tile([P, P], BF16, name="bps", tag="bank")
-            nc.tensor.transpose(out=bps[:], in_=bst[:], identity=identb[:])
-            nc.vector.tensor_scalar(out=bh[:], in0=bps[:, 0:8], scalar1=0.5, scalar2=None, op0=ALU.mult)
-
-        def load_rows(nm, a, i0, i1):
-            nc.sync.dma_start(out=t[nm, a][:, i0:i1, :], in_=rows[nm][:, 2 * a + i0 : 2 * a + i1, :])
-
-        def load_w(g, hh):
-            if hh is None:
-                nc.sync.dma_start(out=raw[g][:], in_=wsrc[g])
-            else:
-                nc.sync.dma_start(out=raw[g, hh][:], in_=wsrc[g][:, :, 512 * hh : 512 * (hh + 1)])
-
-        def ln(k):
-            i0, i1 = LN_UNITS[k]
-            a = i0 // 2
+        def log_n(first, last):
+            a = first // 2
             nc.scalar.activation(
-                out=lr[a][:, i0 - 2 * a : i1 - 2 * a, :], in_=t["n", a][:, i0 - 2 * a : i1 - 2 * a, :], func=ACT.Ln, bias=2e-6, scale=2.0
+                out=recip[a][:, first - 2 * a : last - 2 * a, :],
+                in_=rows["n", a][:, first - 2 * a : last - 2 * a, :],
+                func=ACT.Ln,
+                bias=2.0 * EPS,
+                scale=2.0,
             )
 
-        def ex(a):
-            nc.scalar.activation(out=lr[a][:], in_=lr[a][:], func=ACT.Exp, scale=-1.0)
+        def exp_minus(a):
+            nc.scalar.activation(out=recip[a][:], in_=recip[a][:], func=ACT.Exp, scale=-1.0)
 
-        def cr(a):
-            nc.vector.tensor_tensor(out=crh[a][:], in0=t["c", a][:], in1=lr[a][:], op=ALU.mult)
+        def c_over_n(a):
+            nc.vector.tensor_tensor(out=ratio[a][:], in0=rows["c", a][:], in1=recip[a][:], op=ALU.mult)
 
-        def tx(g, a):
-            words = t["x" if g < 2 else "h", a][:].rearrange("p i k -> p (i k)").bitcast(F32)
-            ps = psum.tile([P, 2, 2, P], F32, name="tx%d%d" % (g, a), tag="bank")
-            for il in range(2):
-                for u in range(2):
-                    lo = 512 * il + 256 * (g % 2)
-                    nc.tensor.transpose(out=ps[:, il, u, :], in_=words[:, lo + u : lo + 256 : 2], identity=ident[:])
-            bank["tx", g, a] = ps
+        def group_weights(k):
+            g, lo, hi, scalar_cols = PIECES[k]
+            cut = hi - lo - scalar_cols
+            nc.vector.tensor_copy(out=w_grouped[k][:, 0:cut, :], in_=w_raw[k][:, :, 0:cut].rearrange("p t m -> p m t"))
+            if scalar_cols:
+                nc.scalar.copy(out=w_grouped[k][:, cut:, :], in_=w_raw[k][:, :, cut:].rearrange("p t m -> p m t"))
 
-        def ev(g, a, eng):
-            dst = xil[g // 2][:, g % 2, :, :].rearrange("p b t -> p (b t)").bitcast(F32)[:, 512 * a : 512 * (a + 1)]
-            dst = dst.rearrange("p (i r u) -> p i r u", i=2, u=2)
-            src = bank["tx", g, a][:].rearrange("p i u r -> p i r u")
-            if eng == "V":
-                nc.vector.tensor_copy(out=dst, in_=src)
-            else:
-                nc.scalar.copy(out=dst, in_=src)
-
-        def qx(gp):
+        def quantise_weights(k):
             nc.vector.quantize_mx(
-                out=xc[gp][:].rearrange("p g b -> p (g b)").bitcast(FP8X4),
-                scales=xs[gp][:].rearrange("p g b -> p (g b)"),
-                in_=xil[gp][:].rearrange("p g b t -> p (g b t)"),
+                out=w_codes[k][:].bitcast(FP8X4), scales=w_scales[k][:], in_=w_grouped[k][:].rearrange("p m t -> p (m t)")
             )
 
-        def il(k, eng):
-            g, c0, c1 = CHUNKS[k]
-            v = VCOLS[k]
-            lo, hi = (0, v) if eng == "V" else (v, c1 - c0)
-            if g in WSPLIT:
-                src = raw[g, c0 // 512][:, :, lo:hi]
-            else:
-                src = raw[g][:, :, c0 + lo : c0 + hi]
-            src = src.rearrange("p t (c i) -> p c t i", i=4)
-            dst = wil[k][:, lo:hi, :].rearrange("p (c i) t -> p c t i", i=4)
-            if eng == "V":
+        def transpose_rows(g, a):
+            words = rows["x" if g < 2 else "h", a][:].rearrange("p i k -> p (i k)").bitcast(F32)
+            turned = psum.tile([P, 2, 2, P], F32, name="turned%d%d" % (g, a), tag="bank")
+            for i in range(2):
+                start = (D_IN // 2) * i + (K_PASS // 2) * (g % 2)
+                for u in range(2):
+                    nc.tensor.transpose(
+                        out=turned[:, i, u, :], in_=words[:, start + u : start + K_PASS // 2 : 2], identity=ident_f32[:]
+                    )
+            bank["turned", g, a] = turned
+
+        def group_rows(g, a, engine):
+            words = a_grouped[g // 2][:, g % 2, :, :].rearrange("p b t -> p (b t)").bitcast(F32)
+            dst = words[:, B * a : B * (a + 1)].rearrange("p (i r u) -> p i r u", i=2, u=2)
+            src = bank["turned", g, a][:].rearrange("p i u r -> p i r u")
+            if engine == "vector":
                 nc.vector.tensor_copy(out=dst, in_=src)
             else:
                 nc.scalar.copy(out=dst, in_=src)
 
-        def qw(k):
-            nc.vector.quantize_mx(out=wc[k][:].bitcast(FP8X4), scales=ws[k][:], in_=wil[k][:].rearrange("p m j -> p (m j)"))
+        def quantise_rows(j):
+            nc.vector.quantize_mx(
+                out=a_codes[j][:].rearrange("p g b -> p (g b)").bitcast(FP8X4),
+                scales=a_scales[j][:].rearrange("p g b -> p (g b)"),
+                in_=a_grouped[j][:].rearrange("p g b t -> p (g b t)"),
+            )
 
-        def mx(g, ct):
+        def multiply(g, ct):
             if g == 0:
-                acc = psum.tile([P, 512], F32, name="acc%d" % ct, tag="bank")
+                acc = psum.tile([P, B], F32, name="acc%d" % ct, tag="bank")
                 bank["acc", ct] = acc
-            k, off = where[g, ct]
+            k, col = piece_of[g, ct]
             nc.tensor.matmul_mx(
                 out=bank["acc", ct][:],
-                lhsT=wc[k][:, off : off + P].bitcast(FP8X4),
-                lhsT_scale=ws[k][:, off : off + P],
-                rhs=xc[g // 2][:, g % 2, :].bitcast(FP8X4),
-                rhs_scale=xs[g // 2][:, g % 2, :],
+                lhsT=w_codes[k][:, col : col + P].bitcast(FP8X4),
+                lhsT_scale=w_scales[k][:, col : col + P],
+                rhs=a_codes[g // 2][:, g % 2, :].bitcast(FP8X4),
+                rhs_scale=a_scales[g // 2][:, g % 2, :],
                 start=(g == 0),
                 stop=(g == 3),
             )
 
-        def th(ct):
-            nc.scalar.activation(out=ot[ct][:], in_=bank["acc", ct][:], func=ACT.Tanh, bias=bh[:, ct : ct + 1], scale=0.5)
+        def tanh_half(ct):
+            nc.scalar.activation(
+                out=tanh_t[ct][:], in_=bank["acc", ct][:], func=ACT.Tanh, bias=half_bias[:, ct : ct + 1], scale=0.5
+            )
 
-        def to(q, a):
-            ps = psum.tile([P, 2, 256], F32, name="to%d%d" % (q, a), tag="bank")
-            for cl in range(2):
-                for il_ in range(2):
-                    i = 2 * a + il_
-                    nc.tensor.transpose(out=ps[:, il_, P * cl : P * (cl + 1)], in_=ot[2 * q + cl][:, P * i : P * (i + 1)], identity=ident[:])
-            bank["to", q, a] = ps
+        def transpose_back(q, a):
+            back = psum.tile([P, 2, QUARTER], F32, name="back%d%d" % (q, a), tag="bank")
+            for half in range(2):
+                for i in range(2):
+                    col = P * (2 * a + i)
+                    nc.tensor.transpose(
+                        out=back[:, i, P * half : P * (half + 1)], in_=tanh_t[2 * q + half][:, col : col + P], identity=ident_f32[:]
+                    )
+            bank["back", q, a] = back
 
-        def fin(q, a):
+        def finish(q, a):
             nc.vector.scalar_tensor_tensor(
-                out=hq[q][:, 2 * a : 2 * a + 2, :],
-                in0=bank["to", q, a][:],
+                out=h_sb[q][:, 2 * a : 2 * a + 2, :],
+                in0=bank["back", q, a][:],
                 scalar=1.0,
-                in1=crh[a][:, :, 256 * q : 256 * (q + 1)],
+                in1=ratio[a][:, :, QUARTER * q : QUARTER * (q + 1)],
                 op0=ALU.add,
                 op1=ALU.mult,
             )
 
-        def c8(q, a, eng):
-            dst = f8[q][:, 2 * a : 2 * a + 2, :].rearrange("p i m -> p (i m)")
-            src = hq[q][:, 2 * a : 2 * a + 2, :].rearrange("p i m -> p (i m)")
-            if eng == "V":
+        def to_bytes(q, a):
+            dst = bytes_sb[q][:, 2 * a : 2 * a + 2, :].rearrange("p i m -> p (i m)")
+            src = h_sb[q][:, 2 * a : 2 * a + 2, :].rearrange("p i m -> p (i m)")
+            if a == 0:
                 nc.vector.tensor_scalar(out=dst, in0=src, scalar1=Y_SCALE, scalar2=None, op0=ALU.mult, saturate=False)
             else:
                 nc.scalar.activation(out=dst, in_=src, func=ACT.Copy, scale=Y_SCALE, saturate=False)
 
-        def st0(q, a):
-            nc.sync.dma_start(out=o0[:, 2 * a : 2 * a + 2, 256 * q : 256 * (q + 1)], in_=hq[q][:, 2 * a : 2 * a + 2, :])
+        def store_h(q, a):
+            nc.sync.dma_start(
+                out=out_0_by_slot[:, 2 * a : 2 * a + 2, QUARTER * q : QUARTER * (q + 1)], in_=h_sb[q][:, 2 * a : 2 * a + 2, :]
+            )
 
-        def st1(q, a):
-            nc.sync.dma_start(out=o1[:, 2 * a : 2 * a + 2, 256 * q : 256 * (q + 1)], in_=f8[q][:, 2 * a : 2 * a + 2, :].bitcast(U8))
+        def store_bytes(q, a):
+            nc.sync.dma_start(
+                out=out_1_by_slot[:, 2 * a : 2 * a + 2, QUARTER * q : QUARTER * (q + 1)],
+                in_=bytes_sb[q][:, 2 * a : 2 * a + 2, :].bitcast(U8),
+            )
 
-        for tok in ORDER.split():
-            op = tok[0:2]
-            d = [int(ch) for ch in tok[2:]]
-            if op == "SU":
-                setup()
-            elif op == "LB":
-                load_bias()
-            elif op == "BI":
-                bias()
-            elif op in ("Lx", "Lh", "Lc", "Ln"):
-                if len(d) == 1:
-                    load_rows(op[1], d[0], 0, 2)
-                else:
-                    load_rows(op[1], d[0], d[1], d[1] + 1)
-            elif op == "LW":
-                load_w(d[0], d[1] if len(d) > 1 else None)
-            elif op == "LN":
-                ln(d[0])
-            elif op == "EX":
-                ex(d[0])
-            elif op == "CR":
-                cr(d[0])
-            elif op == "TX":
-                tx(d[0], d[1])
-            elif op in ("EV", "ES"):
-                ev(d[0], d[1], op[1])
-            elif op == "QX":
-                qx(d[0])
-            elif op in ("IV", "IS"):
-                il(d[0], op[1])
-            elif op == "QW":
-                qw(d[0])
-            elif op == "MX":
-                mx(d[0], d[1])
-            elif op == "TH":
-                th(d[0])
-            elif op == "TO":
-                to(d[0], d[1])
-            elif op == "FI":
-                fin(d[0], d[1])
-            elif op in ("CV", "CS"):
-                c8(d[0], d[1], op[1])
-            elif op == "SA":
-                st0(d[0], d[1])
-            elif op == "SB":
-                st1(d[0], d[1])
-            else:
-                assert False, tok
+        load_rows("n", 2, 4)
+        load_weights(0)
+        nc.vector.memset(one[:], 1.0)
+        nc.scalar.activation(out=unused[:], in_=one[:], func=ACT.Ln)
+        nc.gpsimd.memset(bias_rows[:], 0.0)
+        make_identity(nc, ident_f32[:])
+        make_identity(nc, ident_bf16[:])
+        load_rows("n", 0, 1)
+        load_rows("n", 1, 2)
+        load_weights(1)
+        load_weights(2)
+        nc.sync.dma_start(out=bias_rows[0:8, :], in_=b_o.rearrange("(ct p) -> ct p", p=P))
+        load_rows("x", 0, 2)
+        load_rows("x", 2, 4)
+        load_rows("c", 2, 4)
+        load_rows("h", 0, 2)
+        load_rows("h", 2, 4)
+        load_weights(3)
+        load_rows("c", 0, 2)
+        load_weights(4)
+        load_weights(5)
+
+        log_n(2, 4)
+        group_weights(0)
+        log_n(0, 1)
+        quantise_weights(0)
+        log_n(1, 2)
+        group_weights(1)
+        quantise_weights(1)
+        group_weights(2)
+        exp_minus(1)
+
+        bias_t = psum.tile([P, P], BF16, name="bias_t", tag="bank")
+        nc.tensor.transpose(out=bias_t[:], in_=bias_rows[:], identity=ident_bf16[:])
+        nc.vector.tensor_scalar(out=half_bias[:], in0=bias_t[:, 0:8], scalar1=0.5, scalar2=None, op0=ALU.mult)
+        for a in range(2):
+            for g in (0, 1):
+                transpose_rows(g, a)
+        group_rows(0, 0, "vector")
+        group_rows(1, 0, "scalar")
+        group_rows(0, 1, "scalar")
+        group_rows(1, 1, "scalar")
+        quantise_weights(2)
+        quantise_rows(0)
+        c_over_n(1)
+        for a in range(2):
+            for g in (2, 3):
+                transpose_rows(g, a)
+        exp_minus(0)
+        group_rows(2, 0, "scalar")
+        group_rows(3, 0, "scalar")
+        group_rows(2, 1, "scalar")
+        group_rows(3, 1, "vector")
+
+        for g in (0, 1):
+            for ct in range(8):
+                multiply(g, ct)
+        group_weights(3)
+        quantise_rows(1)
+        quantise_weights(3)
+        group_weights(4)
+        group_weights(5)
+        quantise_weights(4)
+        c_over_n(0)
+        quantise_weights(5)
+        for ct in range(4):
+            multiply(2, ct)
+        for ct in range(4):
+            multiply(3, ct)
+        for ct in range(4, 8):
+            multiply(2, ct)
+
+        for s in range(6):
+            if s < 4:
+                tanh_half(2 * s)
+                tanh_half(2 * s + 1)
+            if s >= 2:
+                to_bytes(s - 2, 1)
+            if 1 <= s <= 4:
+                q = s - 1
+                transpose_back(q, 0)
+                transpose_back(q, 1)
+                if s <= 2:
+                    multiply(3, 2 * (s + 1))
+                    multiply(3, 2 * (s + 1) + 1)
+                finish(q, 0)
+                finish(q, 1)
+                to_bytes(q, 0)
+                store_h(q, 0)
+            if s >= 2:
+                store_bytes(s - 2, 1)
+            if 1 <= s <= 4:
+                store_h(s - 1, 1)
+                store_bytes(s - 1, 0)

@@ -22,15 +22,29 @@ PACK = 4
 K_PASS = P * PACK
 SLOTS = B // P
 QUARTER = 2 * P
+BANK_COLS = 256
 
-PIECES = ((0, 0, 512, 0), (0, 512, 1024, 0), (1, 0, 1024, 0), (2, 0, 1024, 480), (3, 0, 512, 352), (3, 512, 1024, 384))
+HALVES = False
+PIECES = ((0, 0, 512), (0, 512, 1024), (1, 0, 1024), (2, 0, 1024), (3, 0, 512), (3, 512, 1024))
+PLAN = {
+ "D": [("ld","n",2,4),("ldw",0),("ld","n",0,1),("ld","n",1,2),("ldw",1),("ldw",2),("ldb",),("ld","x",0,2),("ld","x",2,4),("ld","c",2,4),("ld","h",0,2),("ld","h",2,4),("ldw",3),("ld","c",0,2),("ldw",4),("ldw",5),
+       ("sth",0,0),("sth",0,1),("stb",0,0),("sth",1,0),("stb",0,1),("sth",1,1),("stb",1,0),("sth",2,0),("stb",1,1),("sth",2,1),("stb",2,0),("sth",3,0),("stb",2,1),("sth",3,1),("stb",3,0),("stb",3,1)],
+ "G": [("consts",)],
+ "S": [("dummy",),("ln",2,4),("ln",0,1),("ln",1,2),("ex",2,4),("gr",1,0),("gr",0,1),("gr",1,1),("ex",0,2),("gr",2,0),("gr",3,0),("gr",2,1),("gw",3,544,1024),("gw",4,160,512),("gw",5,128,512),
+       ("th",0),("th",1),("th",2),("th",3),("th",4),("th",5),("cast",0,1),("th",6),("th",7),("cast",1,1),("cast",2,1),("cast",3,1)],
+ "V": [("one",),("gw",0,0,512),("qw",0,0,512),("gw",1,0,512),("qw",1,0,512),("gw",2,0,1024),("hb",),("gr",0,0),("qw",2,0,1024),("qr",0),("cn",2,4),("gr",3,1),("gw",3,0,544),("qr",1),("qw",3,0,1024),("gw",4,0,160),("gw",5,0,128),("qw",4,0,512),("cn",0,2),("qw",5,0,512),
+       ("fin",0,0),("fin",0,1),("cast",0,0),("fin",1,0),("fin",1,1),("cast",1,0),("fin",2,0),("fin",2,1),("cast",2,0),("fin",3,0),("fin",3,1),("cast",3,0)],
+ "T": [("tb",0),("tr",0,0,1),("tr",1,0,2),("tr",0,1,3),("tr",1,1,4),("tr",2,0,5),("tr",3,0,6),("tr",2,1,7),("tr",3,1,0)]
+      + [("mm",g,ct,(ct+1)%8) for g in (0,1) for ct in range(8)] + [("mm",2,ct,0) for ct in range(4)] + [("mm",3,ct,0) for ct in range(4)] + [("mm",2,ct,0) for ct in range(4,8)]
+      + [("bk",0,0,1),("bk",0,1,2),("mm",3,4,0),("mm",3,5,0),("bk",1,0,3),("bk",1,1,4),("mm",3,6,0),("mm",3,7,0),("bk",2,0,5),("bk",2,1,6),("bk",3,0,7),("bk",3,1,0)],
+}
 
 
 def tile_slstmcell_pb_kernel(tc, x, h_prev, c, n, W_o, b_o, U_o, out_0, out_1):
     nc = tc.nc
     with ExitStack() as ctx:
         keep = ctx.enter_context(tc.tile_pool(name="keep", bufs=1))
-        psum = ctx.enter_context(tc.psum_pool(name="psum", bufs=8))
+        psum = ctx.enter_context(tc.psum_pool(name="psum", bufs=1))
         ctx.enter_context(tc.manual_schedule())
 
         by_slot = {
@@ -52,248 +66,313 @@ def tile_slstmcell_pb_kernel(tc, x, h_prev, c, n, W_o, b_o, U_o, out_0, out_1):
             for a in range(2):
                 rows[name, a] = keep.tile([P, 2, 1024], BF16, name="%s%d" % (name, a))
         w_raw, w_grouped, w_codes, w_scales, piece_of = {}, {}, {}, {}, {}
-        for k, (g, lo, hi, scalar_cols) in enumerate(PIECES):
+        for k, (g, lo, hi) in enumerate(PIECES):
             w_raw[k] = keep.tile([P, PACK, hi - lo], BF16, name="w_raw%d" % k)
             w_grouped[k] = keep.tile([P, hi - lo, PACK], BF16, name="w_grouped%d" % k, align_bytes=64)
             w_codes[k] = keep.tile([P, hi - lo], U32, name="w_codes%d" % k, align_bytes=64)
             w_scales[k] = keep.tile([P, hi - lo], U8, name="w_scales%d" % k, align_bytes=64)
             for ct in range(lo // P, hi // P):
                 piece_of[g, ct] = (k, ct * P - lo)
-        a_grouped, a_codes, a_scales, recip, ratio = {}, {}, {}, {}, {}
+        a_grouped, a_codes, a_scales = {}, {}, {}
         for j in range(2):
             a_grouped[j] = keep.tile([P, 2, B, PACK], BF16, name="a_grouped%d" % j, align_bytes=64)
             a_codes[j] = keep.tile([P, 2, B], U32, name="a_codes%d" % j, align_bytes=64)
             a_scales[j] = keep.tile([P, 2, B], U8, name="a_scales%d" % j, align_bytes=64)
-            recip[j] = keep.tile([P, 2, D_H], F32, name="recip%d" % j)
-            ratio[j] = keep.tile([P, 2, D_H], F32, name="ratio%d" % j)
+        recip, ratio = {}, {}
+        for a in range(2):
+            recip[a] = keep.tile([P, 2, D_H], F32, name="recip%d" % a)
+            ratio[a] = keep.tile([P, 2, D_H], F32, name="ratio%d" % a)
         tanh_t = {}
         for ct in range(8):
             tanh_t[ct] = keep.tile([P, B], F32, name="tanh_t%d" % ct)
-        h_sb, bytes_sb = {}, {}
+        h_sb, bytes_sb, h_half, bytes_half = {}, {}, {}, {}
+        for hf in range(2 if HALVES else 0):
+            for a in range(2):
+                h_half[hf, a] = keep.tile([P, 2, 2 * QUARTER], F32, name="h_half%d%d" % (hf, a))
+                bytes_half[hf, a] = keep.tile([P, 2, 2 * QUARTER], FP8, name="bytes_half%d%d" % (hf, a))
         for q in range(4):
-            h_sb[q] = keep.tile([P, SLOTS, QUARTER], F32, name="h_sb%d" % q)
-            bytes_sb[q] = keep.tile([P, SLOTS, QUARTER], FP8, name="bytes_sb%d" % q)
+            for a in range(2):
+                if HALVES:
+                    h_sb[q, a] = h_half[q // 2, a][:, :, QUARTER * (q % 2) : QUARTER * (q % 2 + 1)]
+                else:
+                    h_q = keep.tile([P, 2, QUARTER], F32, name="h_sb%d%d" % (q, a))
+                    h_sb[q, a] = h_q[:]
+                    bytes_sb[q, a] = keep.tile([P, 2, QUARTER], FP8, name="bytes_sb%d%d" % (q, a))
         ident_f32 = keep.tile([P, P], F32, name="ident_f32")
         ident_bf16 = keep.tile([P, P], BF16, name="ident_bf16")
         bias_rows = keep.tile([P, P], BF16, name="bias_rows")
         half_bias = keep.tile([P, 8], F32, name="half_bias")
         one = keep.tile([P, 1], F32, name="one")
         unused = keep.tile([P, 1], F32, name="unused")
+        waited = keep.tile([P, 1], U32, name="waited")
         bank = {}
 
-        def load_rows(name, first, last):
-            a = first // 2
-            nc.sync.dma_start(out=rows[name, a][:, first - 2 * a : last - 2 * a, :], in_=by_slot[name][:, first:last, :])
-
-        def load_weights(k):
-            g, lo, hi, scalar_cols = PIECES[k]
-            nc.sync.dma_start(out=w_raw[k][:], in_=w_pass[g][:, :, lo:hi])
-
-        def log_n(first, last):
-            a = first // 2
-            nc.scalar.activation(
-                out=recip[a][:, first - 2 * a : last - 2 * a, :],
-                in_=rows["n", a][:, first - 2 * a : last - 2 * a, :],
-                func=ACT.Ln,
-                bias=2.0 * EPS,
-                scale=2.0,
-            )
-
-        def exp_minus(a):
-            nc.scalar.activation(out=recip[a][:], in_=recip[a][:], func=ACT.Exp, scale=-1.0)
-
-        def c_over_n(a):
-            nc.vector.tensor_tensor(out=ratio[a][:], in0=rows["c", a][:], in1=recip[a][:], op=ALU.mult)
-
-        def group_weights(k):
-            g, lo, hi, scalar_cols = PIECES[k]
-            cut = hi - lo - scalar_cols
-            nc.vector.tensor_copy(out=w_grouped[k][:, 0:cut, :], in_=w_raw[k][:, :, 0:cut].rearrange("p t m -> p m t"))
-            if scalar_cols:
-                nc.scalar.copy(out=w_grouped[k][:, cut:, :], in_=w_raw[k][:, :, cut:].rearrange("p t m -> p m t"))
-
-        def quantise_weights(k):
-            nc.vector.quantize_mx(
-                out=w_codes[k][:].bitcast(FP8X4), scales=w_scales[k][:], in_=w_grouped[k][:].rearrange("p m t -> p (m t)")
-            )
-
-        def transpose_rows(g, a):
-            words = rows["x" if g < 2 else "h", a][:].rearrange("p i k -> p (i k)").bitcast(F32)
-            turned = psum.tile([P, 2, 2, P], F32, name="turned%d%d" % (g, a), tag="bank")
-            for i in range(2):
-                start = (D_IN // 2) * i + (K_PASS // 2) * (g % 2)
-                for u in range(2):
-                    nc.tensor.transpose(
-                        out=turned[:, i, u, :], in_=words[:, start + u : start + K_PASS // 2 : 2], identity=ident_f32[:]
-                    )
-            bank["turned", g, a] = turned
-
-        def group_rows(g, a, engine):
-            words = a_grouped[g // 2][:, g % 2, :, :].rearrange("p b t -> p (b t)").bitcast(F32)
-            dst = words[:, B * a : B * (a + 1)].rearrange("p (i r u) -> p i r u", i=2, u=2)
-            src = bank["turned", g, a][:].rearrange("p i u r -> p i r u")
-            if engine == "vector":
-                nc.vector.tensor_copy(out=dst, in_=src)
-            else:
-                nc.scalar.copy(out=dst, in_=src)
-
-        def quantise_rows(j):
-            nc.vector.quantize_mx(
-                out=a_codes[j][:].rearrange("p g b -> p (g b)").bitcast(FP8X4),
-                scales=a_scales[j][:].rearrange("p g b -> p (g b)"),
-                in_=a_grouped[j][:].rearrange("p g b t -> p (g b t)"),
-            )
-
-        def multiply(g, ct):
-            if g == 0:
-                acc = psum.tile([P, B], F32, name="acc%d" % ct, tag="bank")
-                bank["acc", ct] = acc
-            k, col = piece_of[g, ct]
-            nc.tensor.matmul_mx(
-                out=bank["acc", ct][:],
-                lhsT=w_codes[k][:, col : col + P].bitcast(FP8X4),
-                lhsT_scale=w_scales[k][:, col : col + P],
-                rhs=a_codes[g // 2][:, g % 2, :].bitcast(FP8X4),
-                rhs_scale=a_scales[g // 2][:, g % 2, :],
-                start=(g == 0),
-                stop=(g == 3),
-            )
-
-        def tanh_half(ct):
-            nc.scalar.activation(
-                out=tanh_t[ct][:], in_=bank["acc", ct][:], func=ACT.Tanh, bias=half_bias[:, ct : ct + 1], scale=0.5
-            )
-
-        def transpose_back(q, a):
-            back = psum.tile([P, 2, QUARTER], F32, name="back%d%d" % (q, a), tag="bank")
-            for half in range(2):
+        def do(eng, step):
+            op = step[0]
+            if op in ("ld", "ln", "ex", "cn"):
+                f, l = (step[1], step[2]) if op != "ld" else (step[2], step[3])
+                a = f // 2
+                sl = slice(f - 2 * a, l - 2 * a)
+            if op == "ld":
+                nm = step[1]
+                nc.sync.dma_start(out=rows[nm, a][:, sl, :], in_=by_slot[nm][:, f:l, :])
+            elif op == "ldw":
+                k = step[1]
+                g, lo, hi = PIECES[k]
+                nc.sync.dma_start(out=w_raw[k][:], in_=w_pass[g][:, :, lo:hi])
+            elif op == "ldb":
+                nc.sync.dma_start(out=bias_rows[0:8, :], in_=b_o.rearrange("(ct p) -> ct p", p=P))
+            elif op == "sth":
+                q, a = step[1], step[2]
+                nc.sync.dma_start(out=out_0_by_slot[:, 2 * a : 2 * a + 2, QUARTER * q : QUARTER * (q + 1)], in_=h_sb[q, a])
+            elif op == "sth2":
+                hf, a = step[1], step[2]
+                nc.sync.dma_start(out=out_0_by_slot[:, 2 * a : 2 * a + 2, 2 * QUARTER * hf : 2 * QUARTER * (hf + 1)], in_=h_half[hf, a][:])
+            elif op == "stb2":
+                hf, a = step[1], step[2]
+                nc.sync.dma_start(out=out_1_by_slot[:, 2 * a : 2 * a + 2, 2 * QUARTER * hf : 2 * QUARTER * (hf + 1)], in_=bytes_half[hf, a][:].bitcast(U8))
+            elif op == "cast2":
+                hf, a = step[1], step[2]
+                dst = bytes_half[hf, a][:].rearrange("p i m -> p (i m)")
+                src = h_half[hf, a][:].rearrange("p i m -> p (i m)")
+                if eng == "V":
+                    nc.vector.tensor_scalar(out=dst, in0=src, scalar1=Y_SCALE, scalar2=None, op0=ALU.mult, saturate=False)
+                else:
+                    nc.scalar.activation(out=dst, in_=src, func=ACT.Copy, scale=Y_SCALE, saturate=False)
+            elif op == "stb":
+                q, a = step[1], step[2]
+                nc.sync.dma_start(out=out_1_by_slot[:, 2 * a : 2 * a + 2, QUARTER * q : QUARTER * (q + 1)], in_=bytes_sb[q, a][:].bitcast(U8))
+            elif op == "one":
+                nc.vector.memset(one[:], 1.0)
+            elif op == "dummy":
+                nc.scalar.activation(out=unused[:], in_=one[:], func=ACT.Ln)
+            elif op == "consts":
+                nc.gpsimd.memset(bias_rows[:], 0.0)
+                make_identity(nc, ident_f32[:])
+                make_identity(nc, ident_bf16[:])
+            elif op == "ln":
+                nc.scalar.activation(out=recip[a][:, sl, :], in_=rows["n", a][:, sl, :], func=ACT.Ln, bias=2.0 * EPS, scale=2.0)
+            elif op == "ex":
+                nc.scalar.activation(out=recip[a][:, sl, :], in_=recip[a][:, sl, :], func=ACT.Exp, scale=-1.0)
+            elif op == "cn":
+                cols = slice(0, D_H) if len(step) == 3 else slice(QUARTER * step[3], QUARTER * step[4])
+                (nc.vector if eng == "V" else nc.gpsimd).tensor_tensor(out=ratio[a][:, sl, cols], in0=rows["c", a][:, sl, cols], in1=recip[a][:, sl, cols], op=ALU.mult)
+            elif op == "gsync":
+                nc.gpsimd.tensor_copy(out=waited[:], in_=w_codes[step[1]][:, 0:1])
+            elif op == "gw":
+                k, lo, hi = step[1], step[2], step[3]
+                dst, src = w_grouped[k][:, lo:hi, :], w_raw[k][:, :, lo:hi].rearrange("p t m -> p m t")
+                if eng == "V":
+                    nc.vector.tensor_copy(out=dst, in_=src)
+                else:
+                    nc.scalar.copy(out=dst, in_=src)
+            elif op == "pw":
+                k, j, b = step[1], step[2], step[3]
+                passed = psum.tile([P, BANK_COLS * PACK], BF16, name="passed%d%d" % (k, j), tag="bank%d" % b)
+                for half in range(2):
+                    col = BANK_COLS * j + P * half
+                    nc.tensor.matmul(out=passed[:, P * PACK * half : P * PACK * (half + 1)], lhsT=ident_bf16[:],
+                                     rhs=w_raw[k][:, :, col : col + P].rearrange("p t m -> p m t"), start=True, stop=True)
+                bank["passed", k, j] = passed
+            elif op == "wu":
+                k, cnt, b = step[1], step[2], step[3]
+                idle = psum.tile([P, B], F32, name="idle%s" % step[4], tag="bank%d" % b)
+                for r in range(cnt):
+                    nc.tensor.matmul(out=idle[:], lhsT=ident_bf16[:], rhs=w_raw[k][:, r % PACK, 0:B], start=True, stop=True)
+            elif op == "wx":
+                k, cnt, b = step[1], step[2], step[3]
+                idle = psum.tile([P, B], F32, name="idle%s" % step[4], tag="bank%d" % b)
+                for r in range(cnt):
+                    nc.tensor.matmul_mx(out=idle[:], lhsT=w_codes[k][:, 0:P].bitcast(FP8X4), lhsT_scale=w_scales[k][:, 0:P],
+                                        rhs=w_codes[k][:, 0:B].bitcast(FP8X4), rhs_scale=w_scales[k][:, 0:B], start=True, stop=True)
+            elif op == "cp":
+                k, j = step[1], step[2]
+                dst = w_grouped[k][:, BANK_COLS * j : BANK_COLS * (j + 1), :].rearrange("p m t -> p (m t)")
+                if eng == "V":
+                    nc.vector.tensor_copy(out=dst, in_=bank["passed", k, j][:])
+                else:
+                    nc.scalar.copy(out=dst, in_=bank["passed", k, j][:])
+            elif op == "qw":
+                k, lo, hi = step[1], step[2], step[3]
+                nc.vector.quantize_mx(out=w_codes[k][:, lo:hi].bitcast(FP8X4), scales=w_scales[k][:, lo:hi],
+                                      in_=w_grouped[k][:, lo:hi, :].rearrange("p m t -> p (m t)"))
+            elif op == "tb":
+                bias_t = psum.tile([P, P], BF16, name="bias_t", tag="bank%d" % step[1])
+                nc.tensor.transpose(out=bias_t[:], in_=bias_rows[:], identity=ident_bf16[:])
+                bank["bias"] = bias_t
+            elif op == "hb":
+                nc.vector.tensor_scalar(out=half_bias[:], in0=bank["bias"][:, 0:8], scalar1=0.5, scalar2=None, op0=ALU.mult)
+            elif op == "tr":
+                g, a, b = step[1], step[2], step[3]
+                turned = psum.tile([P, 2, 2, P], F32, name="turned%d%d" % (g, a), tag="bank%d" % b)
                 for i in range(2):
-                    col = P * (2 * a + i)
-                    nc.tensor.transpose(
-                        out=back[:, i, P * half : P * (half + 1)], in_=tanh_t[2 * q + half][:, col : col + P], identity=ident_f32[:]
-                    )
-            bank["back", q, a] = back
-
-        def finish(q, a):
-            nc.vector.scalar_tensor_tensor(
-                out=h_sb[q][:, 2 * a : 2 * a + 2, :],
-                in0=bank["back", q, a][:],
-                scalar=1.0,
-                in1=ratio[a][:, :, QUARTER * q : QUARTER * (q + 1)],
-                op0=ALU.add,
-                op1=ALU.mult,
-            )
-
-        def to_bytes(q, a):
-            dst = bytes_sb[q][:, 2 * a : 2 * a + 2, :].rearrange("p i m -> p (i m)")
-            src = h_sb[q][:, 2 * a : 2 * a + 2, :].rearrange("p i m -> p (i m)")
-            if a == 0:
-                nc.vector.tensor_scalar(out=dst, in0=src, scalar1=Y_SCALE, scalar2=None, op0=ALU.mult, saturate=False)
+                    words = rows["x" if g < 2 else "h", a][:, i, :].bitcast(F32)
+                    start = (K_PASS // 2) * (g % 2)
+                    for u in range(2):
+                        nc.tensor.transpose(out=turned[:, i, u, :], in_=words[:, start + u : start + K_PASS // 2 : 2], identity=ident_f32[:])
+                bank["turned", g, a] = turned
+            elif op == "gr":
+                g, a = step[1], step[2]
+                words = a_grouped[g // 2][:, g % 2, :, :].rearrange("p b t -> p (b t)").bitcast(F32)
+                dst = words[:, B * a : B * (a + 1)].rearrange("p (i r u) -> p i r u", i=2, u=2)
+                src = bank["turned", g, a][:].rearrange("p i u r -> p i r u")
+                if eng == "V":
+                    nc.vector.tensor_copy(out=dst, in_=src)
+                else:
+                    nc.scalar.copy(out=dst, in_=src)
+            elif op == "qr":
+                j = step[1]
+                if len(step) == 2:
+                    nc.vector.quantize_mx(out=a_codes[j][:].rearrange("p g b -> p (g b)").bitcast(FP8X4),
+                                          scales=a_scales[j][:].rearrange("p g b -> p (g b)"),
+                                          in_=a_grouped[j][:].rearrange("p g b t -> p (g b t)"))
+                else:
+                    g2 = step[2]
+                    nc.vector.quantize_mx(out=a_codes[j][:, g2, :].bitcast(FP8X4), scales=a_scales[j][:, g2, :],
+                                          in_=a_grouped[j][:, g2, :, :].rearrange("p b t -> p (b t)"))
+            elif op == "mm":
+                g, ct = step[1], step[2]
+                if g == 0:
+                    acc = psum.tile([P, B], F32, name="acc%d" % ct, tag="bank%d" % step[3])
+                    bank["acc", ct] = acc
+                k, col = piece_of[g, ct]
+                nc.tensor.matmul_mx(out=bank["acc", ct][:], lhsT=w_codes[k][:, col : col + P].bitcast(FP8X4),
+                                    lhsT_scale=w_scales[k][:, col : col + P], rhs=a_codes[g // 2][:, g % 2, :].bitcast(FP8X4),
+                                    rhs_scale=a_scales[g // 2][:, g % 2, :], start=(g == 0), stop=(g == 3))
+            elif op == "th":
+                ct = step[1]
+                nc.scalar.activation(out=tanh_t[ct][:], in_=bank["acc", ct][:], func=ACT.Tanh, bias=half_bias[:, ct : ct + 1], scale=0.5)
+            elif op == "bk":
+                q, a, b = step[1], step[2], step[3]
+                back = psum.tile([P, 2, QUARTER], F32, name="back%d%d" % (q, a), tag="bank%d" % b)
+                for half in range(2):
+                    for i in range(2):
+                        col = P * (2 * a + i)
+                        nc.tensor.transpose(out=back[:, i, P * half : P * (half + 1)], in_=tanh_t[2 * q + half][:, col : col + P], identity=ident_f32[:])
+                bank["back", q, a] = back
+            elif op == "fin":
+                q, a = step[1], step[2]
+                nc.vector.scalar_tensor_tensor(out=h_sb[q, a], in0=bank["back", q, a][:], scalar=1.0,
+                                               in1=ratio[a][:, :, QUARTER * q : QUARTER * (q + 1)], op0=ALU.add, op1=ALU.mult)
+            elif op == "cast":
+                q, a = step[1], step[2]
+                dst = bytes_sb[q, a][:].rearrange("p i m -> p (i m)")
+                src = h_sb[q, a].rearrange("p i m -> p (i m)")
+                if eng == "V":
+                    nc.vector.tensor_scalar(out=dst, in0=src, scalar1=Y_SCALE, scalar2=None, op0=ALU.mult, saturate=False)
+                else:
+                    nc.scalar.activation(out=dst, in_=src, func=ACT.Copy, scale=Y_SCALE, saturate=False)
             else:
-                nc.scalar.activation(out=dst, in_=src, func=ACT.Copy, scale=Y_SCALE, saturate=False)
+                raise ValueError(op)
 
-        def store_h(q, a):
-            nc.sync.dma_start(
-                out=out_0_by_slot[:, 2 * a : 2 * a + 2, QUARTER * q : QUARTER * (q + 1)], in_=h_sb[q][:, 2 * a : 2 * a + 2, :]
-            )
+        def needs(step, bank_prev):
+            op = step[0]
+            if op == "sth":
+                return [("fin", step[1], step[2])]
+            if op == "stb":
+                return [("cast", step[1], step[2])]
+            if op == "stb2":
+                return [("cast2", step[1], step[2])]
+            if op in ("cast2", "sth2"):
+                return [("fin", 2 * step[1], step[2]), ("fin", 2 * step[1] + 1, step[2])]
+            if op == "dummy":
+                return [("one",)]
+            if op == "ldb":
+                return [("consts",)]
+            if op == "ln":
+                return [("ld", "n", i) for i in range(step[1], step[2])]
+            if op == "ex":
+                return [("ln", i) for i in range(step[1], step[2])]
+            if op == "cn":
+                return [(o, i) for i in range(step[1], step[2]) for o in ("ex", "ldc")]
+            if op == "gsync":
+                return [s for s in PLAN["V"] if s[0] == "qw" and s[1] == step[1]]
+            if op == "gw":
+                return [("ldw", step[1])]
+            if op == "pw":
+                return [("ldw", step[1]), ("consts",)] + bank_prev.get(step, [])
+            if op == "wu":
+                return [("ldw", step[1]), ("consts",)] + bank_prev.get(step, [])
+            if op == "wx":
+                return [s for s in PLAN["V"] if s[0] == "qw" and s[1] == step[1]] + bank_prev.get(step, [])
+            if op == "cp":
+                return [s for s in PLAN["T"] if s[0] == "pw" and s[1:3] == step[1:3]]
+            if op == "qw":
+                k, lo, hi = step[1], step[2], step[3]
+                out = [s for e in ("V", "S") for s in PLAN[e] if s[0] == "gw" and s[1] == k and s[2] < hi and s[3] > lo]
+                out += [s for e in ("V", "S") for s in PLAN[e] if s[0] == "cp" and s[1] == k and BANK_COLS * s[2] < hi and BANK_COLS * (s[2] + 1) > lo]
+                return out
+            if op == "tb":
+                return [("ldb",), ("consts",)] + bank_prev.get(step, [])
+            if op == "hb":
+                return [s for s in PLAN["T"] if s[0] == "tb"]
+            if op == "tr":
+                nm = "x" if step[1] < 2 else "h"
+                return [("ld", nm, 2 * step[2]), ("ld", nm, 2 * step[2] + 1), ("consts",)] + bank_prev.get(step, [])
+            if op == "gr":
+                return [s for s in PLAN["T"] if s[0] == "tr" and s[1:3] == step[1:3]]
+            if op == "qr":
+                gs = (2 * step[1], 2 * step[1] + 1) if len(step) == 2 else (2 * step[1] + step[2],)
+                return [("gr", g, a) for g in gs for a in range(2)]
+            if op == "mm":
+                g, ct = step[1], step[2]
+                k, col = piece_of[g, ct]
+                out = [s for s in PLAN["V"] if s[0] == "qw" and s[1] == k and s[2] <= col and s[3] >= col + P]
+                out += [s for s in PLAN["V"] if s[0] == "qr" and s[1] == g // 2 and (len(s) == 2 or s[2] == g % 2)]
+                return out + bank_prev.get(step, [])
+            if op == "th":
+                return [s for s in PLAN["T"] if s[0] == "mm" and s[1] == 3 and s[2] == step[1]] + [("hb",)]
+            if op == "bk":
+                return [("th", 2 * step[1]), ("th", 2 * step[1] + 1)] + bank_prev.get(step, [])
+            if op == "fin":
+                return [s for s in PLAN["T"] if s[0] == "bk" and s[1:3] == step[1:3]] + [("cn", 2 * step[2] + i, step[1]) for i in range(2)]
+            if op == "cast":
+                return [("fin", step[1], step[2])]
+            return []
 
-        def store_bytes(q, a):
-            nc.sync.dma_start(
-                out=out_1_by_slot[:, 2 * a : 2 * a + 2, QUARTER * q : QUARTER * (q + 1)],
-                in_=bytes_sb[q][:, 2 * a : 2 * a + 2, :].bitcast(U8),
-            )
+        def reader_of(step):
+            op = step[0]
+            if op == "tb":
+                return ("hb",)
+            if op == "tr":
+                return ("gr", step[1], step[2])
+            if op == "pw":
+                return ("cp", step[1], step[2])
+            if op == "mm":
+                return ("th", step[2])
+            return ("fin", step[1], step[2])
 
-        load_rows("n", 2, 4)
-        load_weights(0)
-        nc.vector.memset(one[:], 1.0)
-        nc.scalar.activation(out=unused[:], in_=one[:], func=ACT.Ln)
-        nc.gpsimd.memset(bias_rows[:], 0.0)
-        make_identity(nc, ident_f32[:])
-        make_identity(nc, ident_bf16[:])
-        load_rows("n", 0, 1)
-        load_rows("n", 1, 2)
-        load_weights(1)
-        load_weights(2)
-        nc.sync.dma_start(out=bias_rows[0:8, :], in_=b_o.rearrange("(ct p) -> ct p", p=P))
-        load_rows("x", 0, 2)
-        load_rows("x", 2, 4)
-        load_rows("c", 2, 4)
-        load_rows("h", 0, 2)
-        load_rows("h", 2, 4)
-        load_weights(3)
-        load_rows("c", 0, 2)
-        load_weights(4)
-        load_weights(5)
-
-        log_n(2, 4)
-        group_weights(0)
-        log_n(0, 1)
-        quantise_weights(0)
-        log_n(1, 2)
-        group_weights(1)
-        quantise_weights(1)
-        group_weights(2)
-        exp_minus(1)
-
-        bias_t = psum.tile([P, P], BF16, name="bias_t", tag="bank")
-        nc.tensor.transpose(out=bias_t[:], in_=bias_rows[:], identity=ident_bf16[:])
-        nc.vector.tensor_scalar(out=half_bias[:], in0=bias_t[:, 0:8], scalar1=0.5, scalar2=None, op0=ALU.mult)
-        for a in range(2):
-            for g in (0, 1):
-                transpose_rows(g, a)
-        group_rows(0, 0, "vector")
-        group_rows(1, 0, "scalar")
-        group_rows(0, 1, "scalar")
-        group_rows(1, 1, "scalar")
-        quantise_weights(2)
-        quantise_rows(0)
-        c_over_n(1)
-        for a in range(2):
-            for g in (2, 3):
-                transpose_rows(g, a)
-        exp_minus(0)
-        group_rows(2, 0, "scalar")
-        group_rows(3, 0, "scalar")
-        group_rows(2, 1, "scalar")
-        group_rows(3, 1, "vector")
-
-        for g in (0, 1):
-            for ct in range(8):
-                multiply(g, ct)
-        group_weights(3)
-        quantise_rows(1)
-        quantise_weights(3)
-        group_weights(4)
-        group_weights(5)
-        quantise_weights(4)
-        c_over_n(0)
-        quantise_weights(5)
-        for ct in range(4):
-            multiply(2, ct)
-        for ct in range(4):
-            multiply(3, ct)
-        for ct in range(4, 8):
-            multiply(2, ct)
-
-        for s in range(6):
-            if s < 4:
-                tanh_half(2 * s)
-                tanh_half(2 * s + 1)
-            if s >= 2:
-                to_bytes(s - 2, 1)
-            if 1 <= s <= 4:
-                q = s - 1
-                transpose_back(q, 0)
-                transpose_back(q, 1)
-                if s <= 2:
-                    multiply(3, 2 * (s + 1))
-                    multiply(3, 2 * (s + 1) + 1)
-                finish(q, 0)
-                finish(q, 1)
-                to_bytes(q, 0)
-                store_h(q, 0)
-            if s >= 2:
-                store_bytes(s - 2, 1)
-            if 1 <= s <= 4:
-                store_h(s - 1, 1)
-                store_bytes(s - 1, 0)
+        bank_prev, last_in_bank = {}, {}
+        for step in PLAN["T"]:
+            if step[0] != "mm" or step[1] == 0:
+                b = step[3] if step[0] in ("wu", "wx") else step[-1]
+                if b in last_in_bank:
+                    bank_prev[step] = [last_in_bank[b]]
+                if step[0] not in ("wu", "wx"):
+                    last_in_bank[b] = reader_of(step)
+        at = dict((e, 0) for e in PLAN)
+        done = set()
+        moved = True
+        while moved:
+            moved = False
+            for e in ("D", "G", "S", "V", "T"):
+                while at[e] < len(PLAN[e]):
+                    step = PLAN[e][at[e]]
+                    if not all(s in done for s in needs(step, bank_prev)):
+                        break
+                    do(e, step)
+                    done.add(step)
+                    if step[0] in ("ln", "ex"):
+                        for i in range(step[1], step[2]):
+                            done.add((step[0], i))
+                    if step[0] == "cn":
+                        for i in range(step[1], step[2]):
+                            for qq in range(4) if len(step) == 3 else range(step[3], step[4]):
+                                done.add(("cn", i, qq))
+                    if step[0] == "ld":
+                        for i in range(step[2], step[3]):
+                            done.add(("ld", step[1], i))
+                            done.add(("ld" + step[1], i))
+                    at[e] += 1
+                    moved = True
+        assert all(at[e] == len(PLAN[e]) for e in PLAN), [(e, PLAN[e][at[e]]) for e in PLAN if at[e] < len(PLAN[e])]

@@ -25,15 +25,16 @@ QUARTER = 2 * P
 BANK_COLS = 256
 
 HALVES = False
+HALVES = True
 PIECES = ((0, 0, 512), (0, 512, 1024), (1, 0, 1024), (2, 0, 1024), (3, 0, 512), (3, 512, 1024))
 PLAN = {
  "D": [("ld","n",2,4),("ldw",0),("ld","n",0,1),("ld","n",1,2),("ldw",1),("ldw",2),("ldb",),("ld","x",0,2),("ld","x",2,4),("ld","c",2,4),("ld","h",0,2),("ld","h",2,4),("ldw",3),("ld","c",0,2),("ldw",4),("ldw",5),
-       ("sth",0,0),("sth",0,1),("stb",0,0),("sth",1,0),("stb",0,1),("sth",1,1),("stb",1,0),("sth",2,0),("stb",1,1),("sth",2,1),("stb",2,0),("sth",3,0),("stb",2,1),("sth",3,1),("stb",3,0),("stb",3,1)],
+       ("sth",0,0),("sth",0,1),("sth",1,0),("sth",1,1),("stb2",0,0),("sth",2,0),("sth",2,1),("stb2",0,1),("sth",3,0),("sth",3,1),("stb2",1,0),("stb2",1,1)],
  "G": [("consts",)],
  "S": [("dummy",),("ln",2,4),("ln",0,1),("ln",1,2),("ex",2,4),("gr",1,0),("gr",0,1),("gr",1,1),("ex",0,2),("gr",2,0),("gr",3,0),("gr",2,1),("gw",3,544,1024),("gw",4,160,512),("gw",5,128,512),
-       ("th",0),("th",1),("th",2),("th",3),("th",4),("th",5),("cast",0,1),("th",6),("th",7),("cast",1,1),("cast",2,1),("cast",3,1)],
+       ("th",0),("th",1),("th",2),("th",3),("th",4),("th",5),("th",6),("th",7),("cast2",0,1),("cast2",1,0)],
  "V": [("one",),("gw",0,0,512),("qw",0,0,512),("gw",1,0,512),("qw",1,0,512),("gw",2,0,1024),("hb",),("gr",0,0),("qw",2,0,1024),("qr",0),("cn",2,4),("gr",3,1),("gw",3,0,544),("qr",1),("qw",3,0,1024),("gw",4,0,160),("gw",5,0,128),("qw",4,0,512),("cn",0,2),("qw",5,0,512),
-       ("fin",0,0),("fin",0,1),("cast",0,0),("fin",1,0),("fin",1,1),("cast",1,0),("fin",2,0),("fin",2,1),("cast",2,0),("fin",3,0),("fin",3,1),("cast",3,0)],
+       ("fin",0,0),("fin",0,1),("fin",1,0),("fin",1,1),("cast2",0,0),("fin",2,0),("fin",2,1),("fin",3,0),("fin",3,1),("cast2",1,1)],
  "T": [("tb",0),("tr",0,0,1),("tr",1,0,2),("tr",0,1,3),("tr",1,1,4),("tr",2,0,5),("tr",3,0,6),("tr",2,1,7),("tr",3,1,0)]
       + [("mm",g,ct,(ct+1)%8) for g in (0,1) for ct in range(8)] + [("mm",2,ct,0) for ct in range(4)] + [("mm",3,ct,0) for ct in range(4)] + [("mm",2,ct,0) for ct in range(4,8)]
       + [("bk",0,0,1),("bk",0,1,2),("mm",3,4,0),("mm",3,5,0),("bk",1,0,3),("bk",1,1,4),("mm",3,6,0),("mm",3,7,0),("bk",2,0,5),("bk",2,1,6),("bk",3,0,7),("bk",3,1,0)],

@@ -31,9 +31,9 @@ PLAN = {
  "D": [("ld","n",2,4),("ldw",0),("ld","n",0,1),("ld","n",1,2),("ldw",1),("ldw",2),("ldb",),("ld","x",0,2),("ld","x",2,4),("ld","c",2,4),("ld","h",0,2),("ld","h",2,4),("ldw",3),("ld","c",0,2),("ldw",4),("ldw",5),
        ("sth",0,0),("sth",0,1),("sth",1,0),("sth",1,1),("stb2",0,0),("sth",2,0),("sth",2,1),("stb2",0,1),("sth",3,0),("sth",3,1),("stb2",1,0),("stb2",1,1)],
  "G": [("consts",)],
- "S": [("dummy",),("ln",2,4),("ln",0,1),("ln",1,2),("ex",2,4),("gr",1,0),("gr",0,1),("gr",1,1),("ex",0,2),("gr",2,0),("gr",3,0),("gr",2,1),("gw",3,544,1024),("gw",4,160,512),("gw",5,128,512),
+ "S": [("dummy",),("ln",2,4),("ln",0,1),("ln",1,2),("ex",2,4),("gr",1,0),("gr",0,1),("gr",1,1),("ex",0,2),("gr",2,0),("gr",3,0),("gr",2,1),("gw",3,512,1024),("gw",4,128,512),("gw",5,64,512),
        ("th",0),("th",1),("th",2),("th",3),("th",4),("th",5),("th",6),("th",7),("cast2",0,1),("cast2",1,0)],
- "V": [("one",),("gw",0,0,512),("qw",0,0,512),("gw",1,0,512),("qw",1,0,512),("gw",2,0,1024),("hb",),("gr",0,0),("qw",2,0,1024),("qr",0),("cn",2,4),("gr",3,1),("gw",3,0,544),("qr",1),("qw",3,0,1024),("gw",4,0,160),("gw",5,0,128),("qw",4,0,512),("cn",0,2),("qw",5,0,512),
+ "V": [("one",),("gw",0,0,512),("qw",0,0,512),("gw",1,0,512),("qw",1,0,512),("gw",2,0,1024),("hb",),("gr",0,0),("qw",2,0,1024),("qr",0),("cn",2,4),("gr",3,1),("gw",3,0,512),("qr",1),("qw",3,0,1024),("gw",4,0,128),("gw",5,0,64),("qw",4,0,512),("cn",0,2),("qw",5,0,512),
        ("fin",0,0),("fin",0,1),("fin",1,0),("fin",1,1),("cast2",0,0),("fin",2,0),("fin",2,1),("fin",3,0),("fin",3,1),("cast2",1,1)],
  "T": [("tb",0),("tr",0,0,1),("tr",1,0,2),("tr",0,1,3),("tr",1,1,4),("tr",2,0,5),("tr",3,0,6),("tr",2,1,7),("tr",3,1,0)]
       + [("mm",g,ct,(ct+1)%8) for g in (0,1) for ct in range(8)] + [("mm",2,ct,0) for ct in range(4)] + [("mm",3,ct,0) for ct in range(4)] + [("mm",2,ct,0) for ct in range(4,8)]
@@ -91,6 +91,9 @@ def tile_slstmcell_pb_kernel(tc, x, h_prev, c, n, W_o, b_o, U_o, out_0, out_1):
             for a in range(2):
                 h_half[hf, a] = keep.tile([P, 2, 2 * QUARTER], F32, name="h_half%d%d" % (hf, a))
                 bytes_half[hf, a] = keep.tile([P, 2, 2 * QUARTER], FP8, name="bytes_half%d%d" % (hf, a))
+        bytes_pair = {}
+        for a in range(2 if HALVES else 0):
+            bytes_pair[a] = keep.tile([P, 2, D_H], FP8, name="bytes_pair%d" % a)
         for q in range(4):
             for a in range(2):
                 if HALVES:
@@ -251,6 +254,39 @@ def tile_slstmcell_pb_kernel(tc, x, h_prev, c, n, W_o, b_o, U_o, out_0, out_1):
                         col = P * (2 * a + i)
                         nc.tensor.transpose(out=back[:, i, P * half : P * (half + 1)], in_=tanh_t[2 * q + half][:, col : col + P], identity=ident_f32[:])
                 bank["back", q, a] = back
+            elif op == "bk2":
+                hf, i, b = step[1], step[2], step[3]
+                back = psum.tile([P, 2 * QUARTER], F32, name="backh%d%d" % (hf, i), tag="bank%d" % b)
+                for j in range(4):
+                    nc.tensor.transpose(out=back[:, P * j : P * (j + 1)], in_=tanh_t[4 * hf + j][:, P * i : P * (i + 1)], identity=ident_f32[:])
+                bank["backh", hf, i] = back
+            elif op == "fin2":
+                hf, i = step[1], step[2]
+                nc.vector.scalar_tensor_tensor(out=h_half[hf, i // 2][:, i % 2, :], in0=bank["backh", hf, i][:], scalar=1.0,
+                                               in1=ratio[i // 2][:, i % 2, 2 * QUARTER * hf : 2 * QUARTER * (hf + 1)], op0=ALU.add, op1=ALU.mult)
+            elif op == "sth3":
+                hf, i = step[1], step[2]
+                nc.sync.dma_start(out=out_0_by_slot[:, i, 2 * QUARTER * hf : 2 * QUARTER * (hf + 1)], in_=h_half[hf, i // 2][:, i % 2, :])
+            elif op == "cast3":
+                hf, i = step[1], step[2]
+                dst, src = bytes_half[hf, i // 2][:, i % 2, :], h_half[hf, i // 2][:, i % 2, :]
+                if eng == "V":
+                    nc.vector.tensor_scalar(out=dst, in0=src, scalar1=Y_SCALE, scalar2=None, op0=ALU.mult, saturate=False)
+                else:
+                    nc.scalar.activation(out=dst, in_=src, func=ACT.Copy, scale=Y_SCALE, saturate=False)
+            elif op == "cast4":
+                hf, i = step[1], step[2]
+                dst, src = bytes_pair[i // 2][:, i % 2, 2 * QUARTER * hf : 2 * QUARTER * (hf + 1)], h_half[hf, i // 2][:, i % 2, :]
+                if eng == "V":
+                    nc.vector.tensor_scalar(out=dst, in0=src, scalar1=Y_SCALE, scalar2=None, op0=ALU.mult, saturate=False)
+                else:
+                    nc.scalar.activation(out=dst, in_=src, func=ACT.Copy, scale=Y_SCALE, saturate=False)
+            elif op == "stb4":
+                a = step[1]
+                nc.sync.dma_start(out=out_1_by_slot[:, 2 * a : 2 * a + 2, :], in_=bytes_pair[a][:].bitcast(U8))
+            elif op == "stb3":
+                hf, i = step[1], step[2]
+                nc.sync.dma_start(out=out_1_by_slot[:, i, 2 * QUARTER * hf : 2 * QUARTER * (hf + 1)], in_=bytes_half[hf, i // 2][:, i % 2, :].bitcast(U8))
             elif op == "fin":
                 q, a = step[1], step[2]
                 nc.vector.scalar_tensor_tensor(out=h_sb[q, a], in0=bank["back", q, a][:], scalar=1.0,
@@ -273,9 +309,21 @@ def tile_slstmcell_pb_kernel(tc, x, h_prev, c, n, W_o, b_o, U_o, out_0, out_1):
             if op == "stb":
                 return [("cast", step[1], step[2])]
             if op == "stb2":
-                return [("cast2", step[1], step[2])]
+                return [s for e in ("V", "S") for s in PLAN[e] if (s[0] == "cast2" and s[1:] == step[1:]) or (s[0] == "cast3" and s[1] == step[1] and s[2] // 2 == step[2])]
             if op in ("cast2", "sth2"):
-                return [("fin", 2 * step[1], step[2]), ("fin", 2 * step[1] + 1, step[2])]
+                return [s for s in PLAN["V"] if (s[0] == "fin" and s[1] // 2 == step[1] and s[2] == step[2]) or (s[0] == "fin2" and s[1] == step[1] and s[2] // 2 == step[2])]
+            if op == "bk2":
+                return [("th", 4 * step[1] + j) for j in range(4)] + bank_prev.get(step, [])
+            if op == "fin2":
+                return [s for s in PLAN["T"] if s[0] == "bk2" and s[1:3] == step[1:3]] + [("cn", step[2], 2 * step[1] + j) for j in range(2)]
+            if op in ("sth3", "cast3"):
+                return [("fin2", step[1], step[2])]
+            if op == "stb3":
+                return [("cast3", step[1], step[2])]
+            if op == "cast4":
+                return [s for s in PLAN["V"] if (s[0] == "fin" and s[1] // 2 == step[1] and s[2] == step[2] // 2) or (s[0] == "fin2" and s[1:] == step[1:])]
+            if op == "stb4":
+                return [("cast4", hf, 2 * step[1] + j) for hf in range(2) for j in range(2)]
             if op == "dummy":
                 return [("one",)]
             if op == "ldb":
@@ -341,6 +389,8 @@ def tile_slstmcell_pb_kernel(tc, x, h_prev, c, n, W_o, b_o, U_o, out_0, out_1):
                 return ("cp", step[1], step[2])
             if op == "mm":
                 return ("th", step[2])
+            if op == "bk2":
+                return ("fin2", step[1], step[2])
             return ("fin", step[1], step[2])
 
         bank_prev, last_in_bank = {}, {}

@@ -28,14 +28,14 @@ HALVES = False
 HALVES = True
 PIECES = ((0, 0, 512), (0, 512, 1024), (1, 0, 1024), (2, 0, 1024), (3, 0, 512), (3, 512, 1024))
 PLAN = {
- "D": [("ld","n",2,4),("ldw",0),("ld","n",0,1),("ld","n",1,2),("ldw",1),("ldw",2),("ldb",),("ld","x",0,2),("ld","x",2,4),("ld","c",2,4),("ld","h",0,2),("ld","h",2,4),("ldw",3),("ld","c",0,2),("ldw",4),("ldw",5),
+ "D": [("ld","n",2,4),("ldw",0),("ld","n",0,2),("ldw",1),("ldw",2),("ld","x",0,2),("ld","x",2,4),("ldb",),("ld","c",2,4),("ld","h",0,2),("ld","h",2,4),("ldw",3),("ld","c",0,2),("ldw",4),("ldw",5),
        ("sth",0,0),("sth",0,1),("sth",1,0),("sth",1,1),("stb2",0,0),("sth",2,0),("sth",2,1),("stb2",0,1),("sth",3,0),("sth",3,1),("stb2",1,0),("stb2",1,1)],
  "G": [("consts",)],
- "S": [("dummy",),("ln",2,4),("ln",0,1),("ln",1,2),("ex",2,4),("gr",1,0),("gr",0,1),("gr",1,1),("ex",0,2),("gr",2,0),("gr",3,0),("gr",2,1),("gw",3,512,1024),("gw",4,128,512),("gw",5,64,512),
+ "S": [("dummy",),("ln",2,4),("ln",0,2),("ex",2,4),("gr",1,0),("gr",0,1),("gr",1,1),("ex",0,2),("gr",2,0),("gr",3,0),("gr",2,1),("gw",3,512,1024),("gw",4,128,512),("gw",5,64,512),
        ("th",0),("th",1),("th",2),("th",3),("th",4),("th",5),("th",6),("th",7),("cast2",0,1),("cast2",1,0)],
- "V": [("one",),("gw",0,0,512),("qw",0,0,512),("gw",1,0,512),("qw",1,0,512),("gw",2,0,1024),("hb",),("gr",0,0),("qw",2,0,1024),("qr",0),("cn",2,4),("gr",3,1),("gw",3,0,512),("qr",1),("qw",3,0,1024),("gw",4,0,128),("gw",5,0,64),("qw",4,0,512),("cn",0,2),("qw",5,0,512),
+ "V": [("one",),("gw",0,0,512),("qw",0,0,512),("gw",1,0,512),("qw",1,0,512),("gw",2,0,1024),("gr",0,0),("qw",2,0,1024),("qr",0),("hb",),("cn",2,4),("gr",3,1),("gw",3,0,512),("qr",1),("qw",3,0,1024),("gw",4,0,128),("gw",5,0,64),("qw",4,0,512),("cn",0,2),("qw",5,0,512),
        ("fin",0,0),("fin",0,1),("fin",1,0),("fin",1,1),("cast2",0,0),("fin",2,0),("fin",2,1),("fin",3,0),("fin",3,1),("cast2",1,1)],
- "T": [("tb",0),("tr",0,0,1),("tr",1,0,2),("tr",0,1,3),("tr",1,1,4),("tr",2,0,5),("tr",3,0,6),("tr",2,1,7),("tr",3,1,0)]
+ "T": [("tr",0,0,1),("tr",1,0,2),("tr",0,1,3),("tr",1,1,4),("tb",0),("tr",2,0,5),("tr",3,0,6),("tr",2,1,7),("tr",3,1,0)]
       + [("mm",g,ct,(ct+1)%8) for g in (0,1) for ct in range(8)] + [("mm",2,ct,0) for ct in range(4)] + [("mm",3,ct,0) for ct in range(4)] + [("mm",2,ct,0) for ct in range(4,8)]
       + [("bk",0,0,1),("bk",0,1,2),("mm",3,4,0),("mm",3,5,0),("bk",1,0,3),("bk",1,1,4),("mm",3,6,0),("mm",3,7,0),("bk",2,0,5),("bk",2,1,6),("bk",3,0,7),("bk",3,1,0)],
 }
@@ -92,7 +92,7 @@ def tile_slstmcell_pb_kernel(tc, x, h_prev, c, n, W_o, b_o, U_o, out_0, out_1):
                 h_half[hf, a] = keep.tile([P, 2, 2 * QUARTER], F32, name="h_half%d%d" % (hf, a))
                 bytes_half[hf, a] = keep.tile([P, 2, 2 * QUARTER], FP8, name="bytes_half%d%d" % (hf, a))
         bytes_pair = {}
-        for a in range(2 if HALVES else 0):
+        for a in range(2 if any(s[0] == "cast4" for e in ("V", "S") for s in PLAN[e]) else 0):
             bytes_pair[a] = keep.tile([P, 2, D_H], FP8, name="bytes_pair%d" % a)
         for q in range(4):
             for a in range(2):

@@ -30,10 +30,10 @@ PIECES = ((0, 0, 512), (0, 512, 1024), (1, 0, 1024), (2, 0, 1024), (3, 0, 512), 
 PLAN = {
  "D": [("ld","n",2,4),("ldw",0),("ld","n",0,2),("ldw",1),("ldw",2),("ld","x",0,2),("ld","x",2,4),("ldb",),("ld","c",2,4),("ld","h",0,2),("ld","h",2,4),("ldw",3),("ld","c",0,2),("ldw",4),("ldw",5),
        ("sth",0,0),("sth",0,1),("sth",1,0),("sth",1,1),("stb2",0,0),("sth",2,0),("sth",2,1),("stb2",0,1),("sth",3,0),("sth",3,1),("stb2",1,0),("stb2",1,1)],
- "G": [("consts",)],
- "S": [("dummy",),("ln",2,4),("ln",0,2),("ex",2,4),("gr",1,0),("gr",0,1),("gr",1,1),("ex",0,2),("gr",2,0),("gr",3,0),("gr",2,1),("gw",3,512,1024),("gw",4,128,512),("gw",5,64,512),
+ "G": [("consts",),("gsync",5),("cn",0,2,3,4),("cn",2,4,3,4)],
+ "S": [("dummy",),("ln",2,4),("ln",0,2),("ex",2,4),("gr",1,0),("gr",0,1),("gr",1,1),("ex",0,2),("gr",2,0),("gr",3,0),("gr",2,1),("gw",3,576,1024),("gw",4,160,512),("gw",5,96,512),
        ("th",0),("th",1),("th",2),("th",3),("th",4),("th",5),("th",6),("th",7),("cast2",0,1),("cast2",1,0)],
- "V": [("one",),("gw",0,0,512),("qw",0,0,512),("gw",1,0,512),("qw",1,0,512),("gw",2,0,1024),("gr",0,0),("qw",2,0,1024),("qr",0),("hb",),("cn",2,4),("gr",3,1),("gw",3,0,512),("qr",1),("qw",3,0,1024),("gw",4,0,128),("gw",5,0,64),("qw",4,0,512),("cn",0,2),("qw",5,0,512),
+ "V": [("one",),("gw",0,0,512),("qw",0,0,512),("gw",1,0,512),("qw",1,0,512),("gw",2,0,1024),("gr",0,0),("qw",2,0,1024),("qr",0),("hb",),("cn",2,4,0,3),("gr",3,1),("gw",3,0,576),("qr",1),("qw",3,0,1024),("gw",4,0,160),("gw",5,0,96),("qw",4,0,512),("cn",0,2,0,3),("qw",5,0,512),
        ("fin",0,0),("fin",0,1),("fin",1,0),("fin",1,1),("cast2",0,0),("fin",2,0),("fin",2,1),("fin",3,0),("fin",3,1),("cast2",1,1)],
  "T": [("tr",0,0,1),("tr",1,0,2),("tr",0,1,3),("tr",1,1,4),("tb",0),("tr",2,0,5),("tr",3,0,6),("tr",2,1,7),("tr",3,1,0)]
       + [("mm",g,ct,(ct+1)%8) for g in (0,1) for ct in range(8)] + [("mm",2,ct,0) for ct in range(4)] + [("mm",3,ct,0) for ct in range(4)] + [("mm",2,ct,0) for ct in range(4,8)]
@@ -87,10 +87,13 @@ def tile_slstmcell_pb_kernel(tc, x, h_prev, c, n, W_o, b_o, U_o, out_0, out_1):
         for ct in range(8):
             tanh_t[ct] = keep.tile([P, B], F32, name="tanh_t%d" % ct)
         h_sb, bytes_sb, h_half, bytes_half = {}, {}, {}, {}
+        h_all, bytes_all = {}, {}
         for hf in range(2 if HALVES else 0):
+            h_all[hf] = keep.tile([P, SLOTS, 2 * QUARTER], F32, name="h_all%d" % hf)
+            bytes_all[hf] = keep.tile([P, SLOTS, 2 * QUARTER], FP8, name="bytes_all%d" % hf)
             for a in range(2):
-                h_half[hf, a] = keep.tile([P, 2, 2 * QUARTER], F32, name="h_half%d%d" % (hf, a))
-                bytes_half[hf, a] = keep.tile([P, 2, 2 * QUARTER], FP8, name="bytes_half%d%d" % (hf, a))
+                h_half[hf, a] = h_all[hf][:, 2 * a : 2 * a + 2, :]
+                bytes_half[hf, a] = bytes_all[hf][:, 2 * a : 2 * a + 2, :]
         bytes_pair = {}
         for a in range(2 if any(s[0] == "cast4" for e in ("V", "S") for s in PLAN[e]) else 0):
             bytes_pair[a] = keep.tile([P, 2, D_H], FP8, name="bytes_pair%d" % a)
@@ -129,6 +132,13 @@ def tile_slstmcell_pb_kernel(tc, x, h_prev, c, n, W_o, b_o, U_o, out_0, out_1):
             elif op == "sth":
                 q, a = step[1], step[2]
                 nc.sync.dma_start(out=out_0_by_slot[:, 2 * a : 2 * a + 2, QUARTER * q : QUARTER * (q + 1)], in_=h_sb[q, a])
+            elif op == "sthq":
+                q = step[1]
+                cols = slice(QUARTER * (q % 2), QUARTER * (q % 2 + 1))
+                nc.sync.dma_start(out=out_0_by_slot[:, :, QUARTER * q : QUARTER * (q + 1)], in_=h_all[q // 2][:, :, cols])
+            elif op == "stbh":
+                hf = step[1]
+                nc.sync.dma_start(out=out_1_by_slot[:, :, 2 * QUARTER * hf : 2 * QUARTER * (hf + 1)], in_=bytes_all[hf][:].bitcast(U8))
             elif op == "sth2":
                 hf, a = step[1], step[2]
                 nc.sync.dma_start(out=out_0_by_slot[:, 2 * a : 2 * a + 2, 2 * QUARTER * hf : 2 * QUARTER * (hf + 1)], in_=h_half[hf, a][:])
@@ -308,6 +318,10 @@ def tile_slstmcell_pb_kernel(tc, x, h_prev, c, n, W_o, b_o, U_o, out_0, out_1):
                 return [("fin", step[1], step[2])]
             if op == "stb":
                 return [("cast", step[1], step[2])]
+            if op == "sthq":
+                return [("fin", step[1], 0), ("fin", step[1], 1)]
+            if op == "stbh":
+                return [("cast2", step[1], 0), ("cast2", step[1], 1)]
             if op == "stb2":
                 return [s for e in ("V", "S") for s in PLAN[e] if (s[0] == "cast2" and s[1:] == step[1:]) or (s[0] == "cast3" and s[1] == step[1] and s[2] // 2 == step[2])]
             if op in ("cast2", "sth2"):

@@ -28,7 +28,7 @@ HALVES = False
 HALVES = True
 PIECES = ((0, 0, 512), (0, 512, 1024), (1, 0, 1024), (2, 0, 1024), (3, 0, 512), (3, 512, 1024))
 PLAN = {
- "D": [("ld","n",2,4),("ldw",0),("ld","n",0,2),("ldw",1),("ldw",2),("ld","x",0,2),("ld","x",2,4),("ldb",),("ld","c",2,4),("ld","h",0,2),("ld","h",2,4),("ldw",3),("ld","c",0,2),("ldw",4),("ldw",5),
+ "D": [("ld","n",2,4),("ldw",0),("ld","n",0,2),("ldw",1),("ldw",2),("ld","x",0,2),("ld","x",2,4),("ldb",),("ld","c",2,4),("ld","h",0,2),("ld","h",2,4),("ldw",3),("ldw",4),("ldw",5),("ld","c",0,2),
        ("sth",0,0),("sth",0,1),("sth",1,0),("sth",1,1),("stb2",0,0),("sth",2,0),("sth",2,1),("stb2",0,1),("sth",3,0),("sth",3,1),("stb2",1,0),("stb2",1,1)],
  "G": [("consts",),("gsync",5),("cn",0,2,3,4),("cn",2,4,3,4)],
  "S": [("dummy",),("ln",2,4),("ln",0,2),("ex",2,4),("gr",1,0),("gr",0,1),("gr",1,1),("ex",0,2),("gr",2,0),("gr",3,0),("gr",2,1),("gw",3,576,1024),("gw",4,160,512),("gw",5,96,512),
@@ -297,6 +297,10 @@ def tile_slstmcell_pb_kernel(tc, x, h_prev, c, n, W_o, b_o, U_o, out_0, out_1):
             elif op == "stb3":
                 hf, i = step[1], step[2]
                 nc.sync.dma_start(out=out_1_by_slot[:, i, 2 * QUARTER * hf : 2 * QUARTER * (hf + 1)], in_=bytes_half[hf, i // 2][:, i % 2, :].bitcast(U8))
+            elif op == "fins":
+                q, i = step[1], step[2]
+                nc.vector.scalar_tensor_tensor(out=h_sb[q, i // 2][:, i % 2, :], in0=bank["back", q, i // 2][:, i % 2, :], scalar=1.0,
+                                               in1=ratio[i // 2][:, i % 2, QUARTER * q : QUARTER * (q + 1)], op0=ALU.add, op1=ALU.mult)
             elif op == "fin":
                 q, a = step[1], step[2]
                 nc.vector.scalar_tensor_tensor(out=h_sb[q, a], in0=bank["back", q, a][:], scalar=1.0,
@@ -315,7 +319,7 @@ def tile_slstmcell_pb_kernel(tc, x, h_prev, c, n, W_o, b_o, U_o, out_0, out_1):
         def needs(step, bank_prev):
             op = step[0]
             if op == "sth":
-                return [("fin", step[1], step[2])]
+                return [s for s in PLAN["V"] if (s[0] == "fin" and s[1:] == step[1:]) or (s[0] == "fins" and s[1] == step[1] and s[2] // 2 == step[2])]
             if op == "stb":
                 return [("cast", step[1], step[2])]
             if op == "sthq":
@@ -330,6 +334,10 @@ def tile_slstmcell_pb_kernel(tc, x, h_prev, c, n, W_o, b_o, U_o, out_0, out_1):
                 return [("th", 4 * step[1] + j) for j in range(4)] + bank_prev.get(step, [])
             if op == "fin2":
                 return [s for s in PLAN["T"] if s[0] == "bk2" and s[1:3] == step[1:3]] + [("cn", step[2], 2 * step[1] + j) for j in range(2)]
+            if op == "fins":
+                return [s for s in PLAN["T"] if s[0] == "bk" and s[1] == step[1] and s[2] == step[2] // 2] + [("cn", step[2], step[1])]
+            if op == "cast3" and ("fin2", step[1], step[2]) not in PLAN["V"]:
+                return [s for s in PLAN["V"] if (s[0] == "fin" and s[1] // 2 == step[1] and s[2] == step[2] // 2) or (s[0] == "fins" and s[1] // 2 == step[1] and s[2] == step[2])]
             if op in ("sth3", "cast3"):
                 return [("fin2", step[1], step[2])]
             if op == "stb3":
@@ -405,6 +413,8 @@ def tile_slstmcell_pb_kernel(tc, x, h_prev, c, n, W_o, b_o, U_o, out_0, out_1):
                 return ("th", step[2])
             if op == "bk2":
                 return ("fin2", step[1], step[2])
+            if ("fin", step[1], step[2]) not in PLAN["V"]:
+                return ("fins", step[1], 2 * step[2] + 1)
             return ("fin", step[1], step[2])
 
         bank_prev, last_in_bank = {}, {}

@@ -29,12 +29,12 @@ HALVES = True
 PIECES = ((0, 0, 512), (0, 512, 1024), (1, 0, 1024), (2, 0, 1024), (3, 0, 512), (3, 512, 1024))
 PLAN = {
  "D": [("ld","n",2,4),("ldw",0),("ld","n",0,2),("ldw",1),("ldw",2),("ld","x",0,2),("ld","x",2,4),("ldb",),("ld","c",2,4),("ld","h",0,2),("ld","h",2,4),("ldw",3),("ldw",4),("ldw",5),("ld","c",0,2),
-       ("sth",0,0),("sth",0,1),("sth",1,0),("sth",1,1),("stb2",0,0),("sth",2,0),("sth",2,1),("stb2",0,1),("sth",3,0),("sth",3,1),("stb2",1,0),("stb2",1,1)],
+       ("sth",0,0),("sth",0,1),("sth",1,0),("sth",1,1),("sth",2,0),("sth",2,1),("sth",3,0),("sth",3,1),("stb4",0),("stb4",1)],
  "G": [("consts",),("gsync",5),("cn",0,2,3,4),("cn",2,4,3,4)],
  "S": [("dummy",),("ln",2,4),("ln",0,2),("ex",2,4),("gr",1,0),("gr",0,1),("gr",1,1),("ex",0,2),("gr",2,0),("gr",3,0),("gr",2,1),("gw",3,576,1024),("gw",4,160,512),("gw",5,96,512),
-       ("th",0),("th",1),("th",2),("th",3),("th",4),("th",5),("th",6),("th",7),("cast2",0,1),("cast2",1,0)],
+       ("th",0),("th",1),("th",2),("th",3),("th",4),("th",5),("th",6),("th",7),("cast4",0,2),("cast4",0,3),("cast4",1,0),("cast4",1,1)],
  "V": [("one",),("gw",0,0,512),("qw",0,0,512),("gw",1,0,512),("qw",1,0,512),("gw",2,0,1024),("gr",0,0),("qw",2,0,1024),("qr",0),("hb",),("cn",2,4,0,3),("gr",3,1),("gw",3,0,576),("qr",1),("qw",3,0,1024),("gw",4,0,160),("gw",5,0,96),("qw",4,0,512),("cn",0,2,0,3),("qw",5,0,512),
-       ("fin",0,0),("fin",0,1),("fin",1,0),("fin",1,1),("cast2",0,0),("fin",2,0),("fin",2,1),("fin",3,0),("fin",3,1),("cast2",1,1)],
+       ("fin",0,0),("fin",0,1),("fin",1,0),("fin",1,1),("cast4",0,0),("cast4",0,1),("fin",2,0),("fin",2,1),("fin",3,0),("fin",3,1),("cast4",1,2),("cast4",1,3)],
  "T": [("tr",0,0,1),("tr",1,0,2),("tr",0,1,3),("tr",1,1,4),("tb",0),("tr",2,0,5),("tr",3,0,6),("tr",2,1,7),("tr",3,1,0)]
       + [("mm",g,ct,(ct+1)%8) for g in (0,1) for ct in range(8)] + [("mm",2,ct,0) for ct in range(4)] + [("mm",3,ct,0) for ct in range(4)] + [("mm",2,ct,0) for ct in range(4,8)]
       + [("bk",0,0,1),("bk",0,1,2),("mm",3,4,0),("mm",3,5,0),("bk",1,0,3),("bk",1,1,4),("mm",3,6,0),("mm",3,7,0),("bk",2,0,5),("bk",2,1,6),("bk",3,0,7),("bk",3,1,0)],

from contextlib import ExitStack

import concourse.mybir as mybir
from concourse.masks import make_identity

F32 = mybir.dt.float32
BF16 = mybir.dt.bfloat16
U32 = mybir.dt.uint32
U8 = mybir.dt.uint8
FP8X4 = mybir.dt.float8_e4m3fn_x4
FP8 = mybir.dt.float8_e4m3fn
ACT = mybir.ActivationFunctionType
ALU = mybir.AluOpType

B, D_IN, D_H = 512, 1024, 1024
FLOPS = 2 * B * (D_IN + D_H) * D_H
Y_SCALE = 350.0
EPS = 1e-6

P = 128
PACK = 4
K_PASS = P * PACK
SLOTS = B // P
QUARTER = 2 * P
BANK_COLS = 256

HALVES = False
HALVES = True
PIECES = ((0, 0, 512), (0, 512, 1024), (1, 0, 1024), (2, 0, 1024), (3, 0, 512), (3, 512, 1024))
PLAN = {
 "D": [("ld","n",2,4),("ldw",0),("ld","n",0,2),("ldw",1),("ldw",2),("ld","x",0,2),("ld","x",2,4),("ldb",),("ld","c",2,4),("ld","h",0,2),("ld","h",2,4),("ldw",3),("ldw",4),("ldw",5),("ld","c",0,2),
       ("sth",0,0),("sth",0,1),("sth",1,0),("sth",1,1),("sth",2,0),("sth",2,1),("sth",3,0),("sth",3,1),("stb4",0),("stb4",1)],
 "G": [("consts",),("gsync",5),("cn",0,2,3,4),("cn",2,4,3,4)],
 "S": [("dummy",),("ln",2,4),("ln",0,2),("ex",2,4),("gr",1,0),("gr",0,1),("gr",1,1),("ex",0,2),("gr",2,0),("gr",3,0),("gr",2,1),("gw",3,576,1024),("gw",4,160,512),("gw",5,96,512),
       ("th",0),("th",1),("th",2),("th",3),("th",4),("th",5),("th",6),("th",7),("cast4",0,2),("cast4",0,3),("cast4",1,0),("cast4",1,1)],
 "V": [("one",),("gw",0,0,512),("qw",0,0,512),("gw",1,0,512),("qw",1,0,512),("gw",2,0,1024),("gr",0,0),("qw",2,0,1024),("qr",0),("hb",),("cn",2,4,0,3),("gr",3,1),("gw",3,0,576),("qr",1),("qw",3,0,1024),("gw",4,0,160),("gw",5,0,96),("qw",4,0,512),("cn",0,2,0,3),("qw",5,0,512),
       ("fin",0,0),("fin",0,1),("fin",1,0),("fin",1,1),("cast4",0,0),("cast4",0,1),("fin",2,0),("fin",2,1),("fin",3,0),("fin",3,1),("cast4",1,2),("cast4",1,3)],
 "T": [("tr",0,0,1),("tr",1,0,2),("tr",0,1,3),("tr",1,1,4),("tb",0),("tr",2,0,5),("tr",3,0,6),("tr",2,1,7),("tr",3,1,0)]
      + [("mm",g,ct,(ct+1)%8) for g in (0,1) for ct in range(8)] + [("mm",2,ct,0) for ct in range(4)] + [("mm",3,ct,0) for ct in range(4)] + [("mm",2,ct,0) for ct in range(4,8)]
      + [("bk",0,0,1),("bk",0,1,2),("mm",3,4,0),("mm",3,5,0),("bk",1,0,3),("bk",1,1,4),("mm",3,6,0),("mm",3,7,0),("bk",2,0,5),("bk",2,1,6),("bk",3,0,7),("bk",3,1,0)],
}


def tile_slstmcell_pb_kernel(tc, x, h_prev, c, n, W_o, b_o, U_o, out_0, out_1):
    nc = tc.nc
    with ExitStack() as ctx:
        keep = ctx.enter_context(tc.tile_pool(name="keep", bufs=1))
        psum = ctx.enter_context(tc.psum_pool(name="psum", bufs=1))
        ctx.enter_context(tc.manual_schedule())

        by_slot = {
            "x": x.rearrange("(p i) k -> p i k", i=SLOTS),
            "h": h_prev.rearrange("(p i) k -> p i k", i=SLOTS),
            "c": c.rearrange("(p i) m -> p i m", i=SLOTS),
            "n": n.rearrange("(p i) m -> p i m", i=SLOTS),
        }
        out_0_by_slot = out_0.rearrange("(p i) m -> p i m", i=SLOTS)
        out_1_by_slot = out_1.rearrange("(p i) m -> p i m", i=SLOTS)
        w_pass = [
            w[K_PASS * half : K_PASS * (half + 1), :].rearrange("(p t) m -> p t m", t=PACK)
            for w in (W_o, U_o)
            for half in range(2)
        ]

        rows = {}
        for name in ("x", "h", "c", "n"):
            for a in range(2):
                rows[name, a] = keep.tile([P, 2, 1024], BF16, name="%s%d" % (name, a))
        w_raw, w_grouped, w_codes, w_scales, piece_of = {}, {}, {}, {}, {}
        for k, (g, lo, hi) in enumerate(PIECES):
            w_raw[k] = keep.tile([P, PACK, hi - lo], BF16, name="w_raw%d" % k)
            w_grouped[k] = keep.tile([P, hi - lo, PACK], BF16, name="w_grouped%d" % k, align_bytes=64)
            w_codes[k] = keep.tile([P, hi - lo], U32, name="w_codes%d" % k, align_bytes=64)
            w_scales[k] = keep.tile([P, hi - lo], U8, name="w_scales%d" % k, align_bytes=64)
            for ct in range(lo // P, hi // P):
                piece_of[g, ct] = (k, ct * P - lo)
        a_grouped, a_codes, a_scales = {}, {}, {}
        for j in range(2):
            a_grouped[j] = keep.tile([P, 2, B, PACK], BF16, name="a_grouped%d" % j, align_bytes=64)
            a_codes[j] = keep.tile([P, 2, B], U32, name="a_codes%d" % j, align_bytes=64)
            a_scales[j] = keep.tile([P, 2, B], U8, name="a_scales%d" % j, align_bytes=64)
        recip, ratio = {}, {}
        for a in range(2):
            recip[a] = keep.tile([P, 2, D_H], F32, name="recip%d" % a)
            ratio[a] = keep.tile([P, 2, D_H], F32, name="ratio%d" % a)
        tanh_t = {}
        for ct in range(8):
            tanh_t[ct] = keep.tile([P, B], F32, name="tanh_t%d" % ct)
        h_sb, bytes_sb, h_half, bytes_half = {}, {}, {}, {}
        h_all, bytes_all = {}, {}
        for hf in range(2 if HALVES else 0):
            h_all[hf] = keep.tile([P, SLOTS, 2 * QUARTER], F32, name="h_all%d" % hf)
            bytes_all[hf] = keep.tile([P, SLOTS, 2 * QUARTER], FP8, name="bytes_all%d" % hf)
            for a in range(2):
                h_half[hf, a] = h_all[hf][:, 2 * a : 2 * a + 2, :]
                bytes_half[hf, a] = bytes_all[hf][:, 2 * a : 2 * a + 2, :]
        bytes_pair = {}
        for a in range(2 if any(s[0] == "cast4" for e in ("V", "S") for s in PLAN[e]) else 0):
            bytes_pair[a] = keep.tile([P, 2, D_H], FP8, name="bytes_pair%d" % a)
        for q in range(4):
            for a in range(2):
                if HALVES:
                    h_sb[q, a] = h_half[q // 2, a][:, :, QUARTER * (q % 2) : QUARTER * (q % 2 + 1)]
                else:
                    h_q = keep.tile([P, 2, QUARTER], F32, name="h_sb%d%d" % (q, a))
                    h_sb[q, a] = h_q[:]
                    bytes_sb[q, a] = keep.tile([P, 2, QUARTER], FP8, name="bytes_sb%d%d" % (q, a))
        ident_f32 = keep.tile([P, P], F32, name="ident_f32")
        ident_bf16 = keep.tile([P, P], BF16, name="ident_bf16")
        bias_rows = keep.tile([P, P], BF16, name="bias_rows")
        half_bias = keep.tile([P, 8], F32, name="half_bias")
        one = keep.tile([P, 1], F32, name="one")
        unused = keep.tile([P, 1], F32, name="unused")
        waited = keep.tile([P, 1], U32, name="waited")
        bank = {}

        def do(eng, step):
            op = step[0]
            if op in ("ld", "ln", "ex", "cn"):
                f, l = (step[1], step[2]) if op != "ld" else (step[2], step[3])
                a = f // 2
                sl = slice(f - 2 * a, l - 2 * a)
            if op == "ld":
                nm = step[1]
                nc.sync.dma_start(out=rows[nm, a][:, sl, :], in_=by_slot[nm][:, f:l, :])
            elif op == "ldw":
                k = step[1]
                g, lo, hi = PIECES[k]
                nc.sync.dma_start(out=w_raw[k][:], in_=w_pass[g][:, :, lo:hi])
            elif op == "ldb":
                nc.sync.dma_start(out=bias_rows[0:8, :], in_=b_o.rearrange("(ct p) -> ct p", p=P))
            elif op == "sth":
                q, a = step[1], step[2]
                nc.sync.dma_start(out=out_0_by_slot[:, 2 * a : 2 * a + 2, QUARTER * q : QUARTER * (q + 1)], in_=h_sb[q, a])
            elif op == "sthq":
                q = step[1]
                cols = slice(QUARTER * (q % 2), QUARTER * (q % 2 + 1))
                nc.sync.dma_start(out=out_0_by_slot[:, :, QUARTER * q : QUARTER * (q + 1)], in_=h_all[q // 2][:, :, cols])
            elif op == "stbh":
                hf = step[1]
                nc.sync.dma_start(out=out_1_by_slot[:, :, 2 * QUARTER * hf : 2 * QUARTER * (hf + 1)], in_=bytes_all[hf][:].bitcast(U8))
            elif op == "sth2":
                hf, a = step[1], step[2]
                nc.sync.dma_start(out=out_0_by_slot[:, 2 * a : 2 * a + 2, 2 * QUARTER * hf : 2 * QUARTER * (hf + 1)], in_=h_half[hf, a][:])
            elif op == "stb2":
                hf, a = step[1], step[2]
                nc.sync.dma_start(out=out_1_by_slot[:, 2 * a : 2 * a + 2, 2 * QUARTER * hf : 2 * QUARTER * (hf + 1)], in_=bytes_half[hf, a][:].bitcast(U8))
            elif op == "cast2":
                hf, a = step[1], step[2]
                dst = bytes_half[hf, a][:].rearrange("p i m -> p (i m)")
                src = h_half[hf, a][:].rearrange("p i m -> p (i m)")
                if eng == "V":
                    nc.vector.tensor_scalar(out=dst, in0=src, scalar1=Y_SCALE, scalar2=None, op0=ALU.mult, saturate=False)
                else:
                    nc.scalar.activation(out=dst, in_=src, func=ACT.Copy, scale=Y_SCALE, saturate=False)
            elif op == "stb":
                q, a = step[1], step[2]
                nc.sync.dma_start(out=out_1_by_slot[:, 2 * a : 2 * a + 2, QUARTER * q : QUARTER * (q + 1)], in_=bytes_sb[q, a][:].bitcast(U8))
            elif op == "one":
                nc.vector.memset(one[:], 1.0)
            elif op == "dummy":
                nc.scalar.activation(out=unused[:], in_=one[:], func=ACT.Ln)
            elif op == "consts":
                nc.gpsimd.memset(bias_rows[:], 0.0)
                make_identity(nc, ident_f32[:])
                make_identity(nc, ident_bf16[:])
            elif op == "ln":
                nc.scalar.activation(out=recip[a][:, sl, :], in_=rows["n", a][:, sl, :], func=ACT.Ln, bias=2.0 * EPS, scale=2.0)
            elif op == "ex":
                nc.scalar.activation(out=recip[a][:, sl, :], in_=recip[a][:, sl, :], func=ACT.Exp, scale=-1.0)
            elif op == "cn":
                cols = slice(0, D_H) if len(step) == 3 else slice(QUARTER * step[3], QUARTER * step[4])
                (nc.vector if eng == "V" else nc.gpsimd).tensor_tensor(out=ratio[a][:, sl, cols], in0=rows["c", a][:, sl, cols], in1=recip[a][:, sl, cols], op=ALU.mult)
            elif op == "gsync":
                nc.gpsimd.tensor_copy(out=waited[:], in_=w_codes[step[1]][:, 0:1])
            elif op == "gw":
                k, lo, hi = step[1], step[2], step[3]
                dst, src = w_grouped[k][:, lo:hi, :], w_raw[k][:, :, lo:hi].rearrange("p t m -> p m t")
                if eng == "V":
                    nc.vector.tensor_copy(out=dst, in_=src)
                else:
                    nc.scalar.copy(out=dst, in_=src)
            elif op == "pw":
                k, j, b = step[1], step[2], step[3]
                passed = psum.tile([P, BANK_COLS * PACK], BF16, name="passed%d%d" % (k, j), tag="bank%d" % b)
                for half in range(2):
                    col = BANK_COLS * j + P * half
                    nc.tensor.matmul(out=passed[:, P * PACK * half : P * PACK * (half + 1)], lhsT=ident_bf16[:],
                                     rhs=w_raw[k][:, :, col : col + P].rearrange("p t m -> p m t"), start=True, stop=True)
                bank["passed", k, j] = passed
            elif op == "wu":
                k, cnt, b = step[1], step[2], step[3]
                idle = psum.tile([P, B], F32, name="idle%s" % step[4], tag="bank%d" % b)
                for r in range(cnt):
                    nc.tensor.matmul(out=idle[:], lhsT=ident_bf16[:], rhs=w_raw[k][:, r % PACK, 0:B], start=True, stop=True)
            elif op == "wx":
                k, cnt, b = step[1], step[2], step[3]
                idle = psum.tile([P, B], F32, name="idle%s" % step[4], tag="bank%d" % b)
                for r in range(cnt):
                    nc.tensor.matmul_mx(out=idle[:], lhsT=w_codes[k][:, 0:P].bitcast(FP8X4), lhsT_scale=w_scales[k][:, 0:P],
                                        rhs=w_codes[k][:, 0:B].bitcast(FP8X4), rhs_scale=w_scales[k][:, 0:B], start=True, stop=True)
            elif op == "cp":
                k, j = step[1], step[2]
                dst = w_grouped[k][:, BANK_COLS * j : BANK_COLS * (j + 1), :].rearrange("p m t -> p (m t)")
                if eng == "V":
                    nc.vector.tensor_copy(out=dst, in_=bank["passed", k, j][:])
                else:
                    nc.scalar.copy(out=dst, in_=bank["passed", k, j][:])
            elif op == "qw":
                k, lo, hi = step[1], step[2], step[3]
                nc.vector.quantize_mx(out=w_codes[k][:, lo:hi].bitcast(FP8X4), scales=w_scales[k][:, lo:hi],
                                      in_=w_grouped[k][:, lo:hi, :].rearrange("p m t -> p (m t)"))
            elif op == "tb":
                bias_t = psum.tile([P, P], BF16, name="bias_t", tag="bank%d" % step[1])
                nc.tensor.transpose(out=bias_t[:], in_=bias_rows[:], identity=ident_bf16[:])
                bank["bias"] = bias_t
            elif op == "hb":
                nc.vector.tensor_scalar(out=half_bias[:], in0=bank["bias"][:, 0:8], scalar1=0.5, scalar2=None, op0=ALU.mult)
            elif op == "tr":
                g, a, b = step[1], step[2], step[3]
                turned = psum.tile([P, 2, 2, P], F32, name="turned%d%d" % (g, a), tag="bank%d" % b)
                for i in range(2):
                    words = rows["x" if g < 2 else "h", a][:, i, :].bitcast(F32)
                    start = (K_PASS // 2) * (g % 2)
                    for u in range(2):
                        nc.tensor.transpose(out=turned[:, i, u, :], in_=words[:, start + u : start + K_PASS // 2 : 2], identity=ident_f32[:])
                bank["turned", g, a] = turned
            elif op == "gr":
                g, a = step[1], step[2]
                words = a_grouped[g // 2][:, g % 2, :, :].rearrange("p b t -> p (b t)").bitcast(F32)
                dst = words[:, B * a : B * (a + 1)].rearrange("p (i r u) -> p i r u", i=2, u=2)
                src = bank["turned", g, a][:].rearrange("p i u r -> p i r u")
                if eng == "V":
                    nc.vector.tensor_copy(out=dst, in_=src)
                else:
                    nc.scalar.copy(out=dst, in_=src)
            elif op == "qr":
                j = step[1]
                if len(step) == 2:
                    nc.vector.quantize_mx(out=a_codes[j][:].rearrange("p g b -> p (g b)").bitcast(FP8X4),
                                          scales=a_scales[j][:].rearrange("p g b -> p (g b)"),
                                          in_=a_grouped[j][:].rearrange("p g b t -> p (g b t)"))
                else:
                    g2 = step[2]
                    nc.vector.quantize_mx(out=a_codes[j][:, g2, :].bitcast(FP8X4), scales=a_scales[j][:, g2, :],
                                          in_=a_grouped[j][:, g2, :, :].rearrange("p b t -> p (b t)"))
            elif op == "mm":
                g, ct = step[1], step[2]
                if g == 0:
                    acc = psum.tile([P, B], F32, name="acc%d" % ct, tag="bank%d" % step[3])
                    bank["acc", ct] = acc
                k, col = piece_of[g, ct]
                nc.tensor.matmul_mx(out=bank["acc", ct][:], lhsT=w_codes[k][:, col : col + P].bitcast(FP8X4),
                                    lhsT_scale=w_scales[k][:, col : col + P], rhs=a_codes[g // 2][:, g % 2, :].bitcast(FP8X4),
                                    rhs_scale=a_scales[g // 2][:, g % 2, :], start=(g == 0), stop=(g == 3))
            elif op == "th":
                ct = step[1]
                nc.scalar.activation(out=tanh_t[ct][:], in_=bank["acc", ct][:], func=ACT.Tanh, bias=half_bias[:, ct : ct + 1], scale=0.5)
            elif op == "bk":
                q, a, b = step[1], step[2], step[3]
                back = psum.tile([P, 2, QUARTER], F32, name="back%d%d" % (q, a), tag="bank%d" % b)
                for half in range(2):
                    for i in range(2):
                        col = P * (2 * a + i)
                        nc.tensor.transpose(out=back[:, i, P * half : P * (half + 1)], in_=tanh_t[2 * q + half][:, col : col + P], identity=ident_f32[:])
                bank["back", q, a] = back
            elif op == "bk2":
                hf, i, b = step[1], step[2], step[3]
                back = psum.tile([P, 2 * QUARTER], F32, name="backh%d%d" % (hf, i), tag="bank%d" % b)
                for j in range(4):
                    nc.tensor.transpose(out=back[:, P * j : P * (j + 1)], in_=tanh_t[4 * hf + j][:, P * i : P * (i + 1)], identity=ident_f32[:])
                bank["backh", hf, i] = back
            elif op == "fin2":
                hf, i = step[1], step[2]
                nc.vector.scalar_tensor_tensor(out=h_half[hf, i // 2][:, i % 2, :], in0=bank["backh", hf, i][:], scalar=1.0,
                                               in1=ratio[i // 2][:, i % 2, 2 * QUARTER * hf : 2 * QUARTER * (hf + 1)], op0=ALU.add, op1=ALU.mult)
            elif op == "sth3":
                hf, i = step[1], step[2]
                nc.sync.dma_start(out=out_0_by_slot[:, i, 2 * QUARTER * hf : 2 * QUARTER * (hf + 1)], in_=h_half[hf, i // 2][:, i % 2, :])
            elif op == "cast3":
                hf, i = step[1], step[2]
                dst, src = bytes_half[hf, i // 2][:, i % 2, :], h_half[hf, i // 2][:, i % 2, :]
                if eng == "V":
                    nc.vector.tensor_scalar(out=dst, in0=src, scalar1=Y_SCALE, scalar2=None, op0=ALU.mult, saturate=False)
                else:
                    nc.scalar.activation(out=dst, in_=src, func=ACT.Copy, scale=Y_SCALE, saturate=False)
            elif op == "cast4":
                hf, i = step[1], step[2]
                dst, src = bytes_pair[i // 2][:, i % 2, 2 * QUARTER * hf : 2 * QUARTER * (hf + 1)], h_half[hf, i // 2][:, i % 2, :]
                if eng == "V":
                    nc.vector.tensor_scalar(out=dst, in0=src, scalar1=Y_SCALE, scalar2=None, op0=ALU.mult, saturate=False)
                else:
                    nc.scalar.activation(out=dst, in_=src, func=ACT.Copy, scale=Y_SCALE, saturate=False)
            elif op == "stb4":
                a = step[1]
                nc.sync.dma_start(out=out_1_by_slot[:, 2 * a : 2 * a + 2, :], in_=bytes_pair[a][:].bitcast(U8))
            elif op == "stb3":
                hf, i = step[1], step[2]
                nc.sync.dma_start(out=out_1_by_slot[:, i, 2 * QUARTER * hf : 2 * QUARTER * (hf + 1)], in_=bytes_half[hf, i // 2][:, i % 2, :].bitcast(U8))
            elif op == "fins":
                q, i = step[1], step[2]
                nc.vector.scalar_tensor_tensor(out=h_sb[q, i // 2][:, i % 2, :], in0=bank["back", q, i // 2][:, i % 2, :], scalar=1.0,
                                               in1=ratio[i // 2][:, i % 2, QUARTER * q : QUARTER * (q + 1)], op0=ALU.add, op1=ALU.mult)
            elif op == "fin":
                q, a = step[1], step[2]
                nc.vector.scalar_tensor_tensor(out=h_sb[q, a], in0=bank["back", q, a][:], scalar=1.0,
                                               in1=ratio[a][:, :, QUARTER * q : QUARTER * (q + 1)], op0=ALU.add, op1=ALU.mult)
            elif op == "cast":
                q, a = step[1], step[2]
                dst = bytes_sb[q, a][:].rearrange("p i m -> p (i m)")
                src = h_sb[q, a].rearrange("p i m -> p (i m)")
                if eng == "V":
                    nc.vector.tensor_scalar(out=dst, in0=src, scalar1=Y_SCALE, scalar2=None, op0=ALU.mult, saturate=False)
                else:
                    nc.scalar.activation(out=dst, in_=src, func=ACT.Copy, scale=Y_SCALE, saturate=False)
            else:
                raise ValueError(op)

        def needs(step, bank_prev):
            op = step[0]
            if op == "sth":
                return [s for s in PLAN["V"] if (s[0] == "fin" and s[1:] == step[1:]) or (s[0] == "fins" and s[1] == step[1] and s[2] // 2 == step[2])]
            if op == "stb":
                return [("cast", step[1], step[2])]
            if op == "sthq":
                return [("fin", step[1], 0), ("fin", step[1], 1)]
            if op == "stbh":
                return [("cast2", step[1], 0), ("cast2", step[1], 1)]
            if op == "stb2":
                return [s for e in ("V", "S") for s in PLAN[e] if (s[0] == "cast2" and s[1:] == step[1:]) or (s[0] == "cast3" and s[1] == step[1] and s[2] // 2 == step[2])]
            if op in ("cast2", "sth2"):
                return [s for s in PLAN["V"] if (s[0] == "fin" and s[1] // 2 == step[1] and s[2] == step[2]) or (s[0] == "fin2" and s[1] == step[1] and s[2] // 2 == step[2])]
            if op == "bk2":
                return [("th", 4 * step[1] + j) for j in range(4)] + bank_prev.get(step, [])
            if op == "fin2":
                return [s for s in PLAN["T"] if s[0] == "bk2" and s[1:3] == step[1:3]] + [("cn", step[2], 2 * step[1] + j) for j in range(2)]
            if op == "fins":
                return [s for s in PLAN["T"] if s[0] == "bk" and s[1] == step[1] and s[2] == step[2] // 2] + [("cn", step[2], step[1])]
            if op == "cast3" and ("fin2", step[1], step[2]) not in PLAN["V"]:
                return [s for s in PLAN["V"] if (s[0] == "fin" and s[1] // 2 == step[1] and s[2] == step[2] // 2) or (s[0] == "fins" and s[1] // 2 == step[1] and s[2] == step[2])]
            if op in ("sth3", "cast3"):
                return [("fin2", step[1], step[2])]
            if op == "stb3":
                return [("cast3", step[1], step[2])]
            if op == "cast4":
                return [s for s in PLAN["V"] if (s[0] == "fin" and s[1] // 2 == step[1] and s[2] == step[2] // 2) or (s[0] == "fin2" and s[1:] == step[1:])]
            if op == "stb4":
                return [("cast4", hf, 2 * step[1] + j) for hf in range(2) for j in range(2)]
            if op == "dummy":
                return [("one",)]
            if op == "ldb":
                return [("consts",)]
            if op == "ln":
                return [("ld", "n", i) for i in range(step[1], step[2])]
            if op == "ex":
                return [("ln", i) for i in range(step[1], step[2])]
            if op == "cn":
                return [(o, i) for i in range(step[1], step[2]) for o in ("ex", "ldc")]
            if op == "gsync":
                return [s for s in PLAN["V"] if s[0] == "qw" and s[1] == step[1]]
            if op == "gw":
                return [("ldw", step[1])]
            if op == "pw":
                return [("ldw", step[1]), ("consts",)] + bank_prev.get(step, [])
            if op == "wu":
                return [("ldw", step[1]), ("consts",)] + bank_prev.get(step, [])
            if op == "wx":
                return [s for s in PLAN["V"] if s[0] == "qw" and s[1] == step[1]] + bank_prev.get(step, [])
            if op == "cp":
                return [s for s in PLAN["T"] if s[0] == "pw" and s[1:3] == step[1:3]]
            if op == "qw":
                k, lo, hi = step[1], step[2], step[3]
                out = [s for e in ("V", "S") for s in PLAN[e] if s[0] == "gw" and s[1] == k and s[2] < hi and s[3] > lo]
                out += [s for e in ("V", "S") for s in PLAN[e] if s[0] == "cp" and s[1] == k and BANK_COLS * s[2] < hi and BANK_COLS * (s[2] + 1) > lo]
                return out
            if op == "tb":
                return [("ldb",), ("consts",)] + bank_prev.get(step, [])
            if op == "hb":
                return [s for s in PLAN["T"] if s[0] == "tb"]
            if op == "tr":
                nm = "x" if step[1] < 2 else "h"
                return [("ld", nm, 2 * step[2]), ("ld", nm, 2 * step[2] + 1), ("consts",)] + bank_prev.get(step, [])
            if op == "gr":
                return [s for s in PLAN["T"] if s[0] == "tr" and s[1:3] == step[1:3]]
            if op == "qr":
                gs = (2 * step[1], 2 * step[1] + 1) if len(step) == 2 else (2 * step[1] + step[2],)
                return [("gr", g, a) for g in gs for a in range(2)]
            if op == "mm":
                g, ct = step[1], step[2]
                k, col = piece_of[g, ct]
                out = [s for s in PLAN["V"] if s[0] == "qw" and s[1] == k and s[2] <= col and s[3] >= col + P]
                out += [s for s in PLAN["V"] if s[0] == "qr" and s[1] == g // 2 and (len(s) == 2 or s[2] == g % 2)]
                return out + bank_prev.get(step, [])
            if op == "th":
                return [s for s in PLAN["T"] if s[0] == "mm" and s[1] == 3 and s[2] == step[1]] + [("hb",)]
            if op == "bk":
                return [("th", 2 * step[1]), ("th", 2 * step[1] + 1)] + bank_prev.get(step, [])
            if op == "fin":
                return [s for s in PLAN["T"] if s[0] == "bk" and s[1:3] == step[1:3]] + [("cn", 2 * step[2] + i, step[1]) for i in range(2)]
            if op == "cast":
                return [("fin", step[1], step[2])]
            return []

        def reader_of(step):
            op = step[0]
            if op == "tb":
                return ("hb",)
            if op == "tr":
                return ("gr", step[1], step[2])
            if op == "pw":
                return ("cp", step[1], step[2])
            if op == "mm":
                return ("th", step[2])
            if op == "bk2":
                return ("fin2", step[1], step[2])
            if ("fin", step[1], step[2]) not in PLAN["V"]:
                return ("fins", step[1], 2 * step[2] + 1)
            return ("fin", step[1], step[2])

        bank_prev, last_in_bank = {}, {}
        for step in PLAN["T"]:
            if step[0] != "mm" or step[1] == 0:
                b = step[3] if step[0] in ("wu", "wx") else step[-1]
                if b in last_in_bank:
                    bank_prev[step] = [last_in_bank[b]]
                if step[0] not in ("wu", "wx"):
                    last_in_bank[b] = reader_of(step)
        at = dict((e, 0) for e in PLAN)
        done = set()
        moved = True
        while moved:
            moved = False
            for e in ("D", "G", "S", "V", "T"):
                while at[e] < len(PLAN[e]):
                    step = PLAN[e][at[e]]
                    if not all(s in done for s in needs(step, bank_prev)):
                        break
                    do(e, step)
                    done.add(step)
                    if step[0] in ("ln", "ex"):
                        for i in range(step[1], step[2]):
                            done.add((step[0], i))
                    if step[0] == "cn":
                        for i in range(step[1], step[2]):
                            for qq in range(4) if len(step) == 3 else range(step[3], step[4]):
                                done.add(("cn", i, qq))
                    if step[0] == "ld":
                        for i in range(step[2], step[3]):
                            done.add(("ld", step[1], i))
                            done.add(("ld" + step[1], i))
                    at[e] += 1
                    moved = True
        assert all(at[e] == len(PLAN[e]) for e in PLAN), [(e, PLAN[e][at[e]]) for e in PLAN if at[e] < len(PLAN[e])]
